import numpy as np
import ml_dtypes


def mxq(x, axis, fmt="e4m3"):
    dtype, down = {"e4m3": (ml_dtypes.float8_e4m3fn, 7), "e5m2": (ml_dtypes.float8_e5m2, 14)}[fmt]
    v = np.moveaxis(np.asarray(x, np.float32).astype(ml_dtypes.bfloat16).astype(np.float64), axis, -1)
    blocks = v.reshape(v.shape[:-1] + (-1, 32))
    amax = np.abs(blocks).max(-1, keepdims=True)
    byte = np.maximum(np.where(amax > 0, np.frexp(amax)[1] - 1 + 127, 0) - down, 1)
    scale = np.exp2(byte - 127.0)
    codes = (blocks / scale).astype(np.float32).astype(dtype).astype(np.float64)
    return np.moveaxis((codes * scale).reshape(v.shape), -1, axis)


WIDE = False


def mx_kscale(k):
    if not WIDE:
        return np.ones(k)
    levels = np.array([10, -10, 5, -5, 0])
    if k % 512:
        return np.exp2(np.random.permutation(np.resize(levels, k // 32))).repeat(32)
    a = np.empty((k // 512, 16))
    for p in range(k // 512):
        a[p, :8] = np.random.permutation(np.resize(levels, 8))
        for g in range(8):
            far = levels[np.abs(levels - a[p, g]) >= 10]
            a[p, g + 8] = far[np.random.randint(len(far))]
    return np.exp2(a.ravel()).repeat(32)


BF16 = ml_dtypes.bfloat16


def bf(x):
    return np.asarray(x, np.float32).astype(BF16)


def f64(x):
    return np.asarray(x).astype(np.float64)


B, T, C, H, NOPE, ROPE, VD, LORA = 1, 512, 2048, 16, 128, 128, 128, 512
QK = NOPE + ROPE
HALF = ROPE // 2


def make_freq_cis():
    inv = 1.0 / (10000.0 ** (np.arange(0, ROPE, 2) / ROPE))
    ang = np.outer(np.arange(T), inv)
    return np.stack([np.cos(ang), np.sin(ang)], -1)


def apply_rope(v, fc):
    vr = v.reshape(B, T, H, HALF, 2)
    f = fc.reshape(1, T, 1, HALF, 2)
    real = vr[..., 0] * f[..., 0] - vr[..., 1] * f[..., 1]
    imag = vr[..., 1] * f[..., 0] + vr[..., 0] * f[..., 1]
    return np.stack([real, imag], -1).reshape(B, T, H, ROPE)


def draw0():
    s = mx_kscale(C)
    return {"x": bf(np.random.standard_normal((B, T, C)) * s),
            "freq_cis": bf(make_freq_cis()),
            "Wq": bf(np.random.standard_normal((C, H * QK)) * 2.0 / np.sqrt(C) / s[:, None])}


def core(x, freq_cis, Wq):
    q = (mxq(f64(x), 2, "e4m3") @ mxq(f64(Wq), 0, "e4m3")).reshape(B, T, H, QK)
    q_nope, q_rope = q[..., :NOPE], q[..., NOPE:]
    q_rope = apply_rope(q_rope, f64(freq_cis))
    return np.concatenate([q_nope, q_rope], -1)


def e4m3fn_bytes(y):
    return np.clip(np.asarray(y, np.float64), -448.0, 448.0).astype(np.float32).astype(ml_dtypes.float8_e4m3fn).view(np.uint8)


def e4m3fn_values(b):
    return np.asarray(b, np.uint8).view(ml_dtypes.float8_e4m3fn).astype(np.float64)


def setup_inputs():
    d = draw0()
    x0 = np.asarray(d['Wq']).astype(np.float64)
    s = (np.max(np.abs(x0), axis=(1,), keepdims=True) / 448.0).astype(np.float32)
    out = {}
    for k, v in d.items():
        if k == 'Wq':
            out['Wq_bytes'] = e4m3fn_bytes(x0 / s.astype(np.float64))
            out['Wq_scale'] = s
        else:
            out[k] = v
    return out


def reference(x, freq_cis, Wq_bytes, Wq_scale):
    return core(x, freq_cis, e4m3fn_values(Wq_bytes) * Wq_scale.astype(np.float64))

@@ -1,0 +1,285 @@
+from contextlib import ExitStack
+
+import concourse.mybir as mybir
+from concourse.masks import make_identity
+
+F32 = mybir.dt.float32
+BF16 = mybir.dt.bfloat16
+U32 = mybir.dt.uint32
+U8 = mybir.dt.uint8
+FP8 = mybir.dt.float8_e4m3fn
+FP8X4 = mybir.dt.float8_e4m3fn_x4
+MULT = mybir.AluOpType.mult
+ADD = mybir.AluOpType.add
+COPY = mybir.ActivationFunctionType.Copy
+
+P = 128
+T = 512
+K = 2048
+HEADS = 16
+HD = 256
+G = K // 512
+MT = T // P
+QUADS = 4
+UNITS = QUADS * G
+NOPE, ROPE = 0, 1
+LEAD = 3
+S_LEAD = 2
+GPSIMD_ADDS = 3
+X_STEP = (2, 2, 3, 3)
+TABLE_STEP = 3
+VECTOR_PLANES = ((0, 2), (0, 3), (1, 2), (1, 3))
+SCALAR_BLOCKS = ((9, NOPE), (12, NOPE), (13, NOPE), (14, NOPE), (15, NOPE))
+
+WOVEN_UNITS = (13, 14)
+WOVEN = {1: 13, 3: 14}
+
+FLOPS = 2 * T * K * HEADS * HD
+
+
+def tile_multiheadlatentattention_pb_kernel(tc, x, freq_cis, Wq_bytes, Wq_scale, out):
+    nc = tc.nc
+    w_view = Wq_bytes.rearrange("(g p t) n -> g p t n", p=P, t=4)
+    x_view = x.rearrange("b (m p) k -> (b m) p k", p=P)
+    out_view = out.rearrange("b (m p) h d -> (b m) p h d", p=P)
+
+    with ExitStack() as ctx:
+        ctx.enter_context(tc.manual_schedule())
+        const = ctx.enter_context(tc.tile_pool(name="const", bufs=1))
+        wb_pool = ctx.enter_context(tc.tile_pool(name="wbytes", bufs=UNITS))
+        pl_pool = ctx.enter_context(tc.tile_pool(name="planes", bufs=6))
+        gr_pool = ctx.enter_context(tc.tile_pool(name="grouped", bufs=7))
+        wc_pool = ctx.enter_context(tc.tile_pool(name="wcodes", bufs=10))
+        psum = ctx.enter_context(tc.psum_pool(name="psum", bufs=8))
+
+        wsc = const.tile([P, G, 4], F32, name="wsc")
+        nc.scalar.dma_start(out=wsc[:], in_=Wq_scale.rearrange("(g p t) o -> p g (t o)", p=P, t=4))
+        warm = const.tile([P, 2], F32, name="warm")
+        nc.vector.memset(warm[:], 0.0)
+        nc.scalar.activation(out=warm[:, 1:2], in_=warm[:, 0:1], func=COPY)
+        ident = const.tile([P, P], F32, name="ident")
+        make_identity(nc, ident[:])
+        fc = const.tile([P, MT, P], BF16, name="fc")
+        cos2 = const.tile([P, MT, P], F32, name="cos2")
+        sin2 = const.tile([P, MT, P], F32, name="sin2")
+        xc = const.tile([P, G, T], U32, name="xc", align_bytes=64)
+        xs = const.tile([P, G, T], U8, name="xs", align_bytes=64)
+
+        wbytes = {}
+
+        def load_w(n):
+            q, g = divmod(n, G)
+            cols = slice(1024 * q, 1024 * (q + 1))
+            wb = wb_pool.tile([P, 4, 1024], U8, name="wb", tag="wb")
+            wbytes[n] = wb
+            if n == 0:
+                for t in range(4):
+                    nc.sync.dma_start(out=wb[:, t, :], in_=w_view[g, :, t, cols])
+            else:
+                nc.sync.dma_start(out=wb[:], in_=w_view[g, :, :, cols])
+
+        planes = {}
+
+        def widen(n):
+            q, g = divmod(n, G)
+            pl = pl_pool.tile([P, 4, 1024], BF16, name="pl", tag="pl")
+            planes[n] = pl
+            for t in range(4):
+                src = wbytes[n][:, t, :].bitcast(FP8)
+                if (n, t) in VECTOR_PLANES:
+                    nc.vector.tensor_scalar(out=pl[:, t, :], in0=src, scalar1=wsc[:, g, t:t + 1],
+                                            scalar2=None, op0=MULT)
+                else:
+                    nc.scalar.activation(out=pl[:, t, :], in_=src, func=COPY, scale=wsc[:, g, t:t + 1])
+
+        grouped = {}
+
+        def interleave(n, s):
+            gr = gr_pool.tile([P, 2048], BF16, name="gr", tag="gr", align_bytes=64)
+            grouped[(n, s)] = gr
+            dst = gr[:].rearrange("p (h a i t) -> p h a t i", h=4, i=4, t=4)
+            src = planes[n][:].rearrange("p t (h s a i) -> p s h a t i", s=2, a=32, i=4)[:, s]
+            if (n, s) in SCALAR_BLOCKS:
+                nc.scalar.copy(out=dst, in_=src)
+            else:
+                nc.vector.tensor_copy(out=dst, in_=src)
+
+        codes = {}
+
+        def quantize(n, s):
+            wc = wc_pool.tile([P, 512], U32, name="wc", tag="wc", align_bytes=64)
+            ws = wc_pool.tile([P, 512], U8, name="ws", tag="ws", align_bytes=64)
+            codes[(n, s)] = (wc, ws)
+            nc.vector.quantize_mx(out=wc[:].bitcast(FP8X4), scales=ws[:], in_=grouped[(n, s)][:])
+
+        acc = {}
+
+        def multiply(n, s):
+            q, g = divmod(n, G)
+            wc, ws = codes[(n, s)]
+            for m in range(MT):
+                if g == 0:
+                    bank = psum.tile([P, 512], F32, name="bank", tag="bank")
+                    acc[(q, s, m)] = bank
+                toks = slice(P * m, P * (m + 1))
+                nc.tensor.matmul_mx(out=acc[(q, s, m)][:],
+                                    lhsT=xc[:, g, toks].bitcast(FP8X4), lhsT_scale=xs[:, g, toks],
+                                    rhs=wc[:].bitcast(FP8X4), rhs_scale=ws[:],
+                                    start=(g == 0), stop=(g == G - 1))
+
+        x_tiles = {}
+
+        def x_turn(m):
+            words = x_tiles[m][:].bitcast(F32)
+            for gp in range(G // 2):
+                xt = psum.tile([P, 2, 2, P], F32, name="xt", tag="bank")
+                for gg in range(2):
+                    g = 2 * gp + gg
+                    for u in range(2):
+                        nc.tensor.transpose(out=xt[:, gg, u, :], in_=words[:, 256 * g + u:256 * (g + 1):2],
+                                            identity=ident[:])
+                nc.vector.tensor_copy(out=x_tiles["xg"][:, 2 * gp:2 * gp + 2, P * m:P * (m + 1), :],
+                                      in_=xt[:].rearrange("p g u r -> p g r u"))
+
+        def x_quantize():
+            for g in range(G):
+                nc.vector.quantize_mx(out=xc[:, g, :].bitcast(FP8X4), scales=xs[:, g, :],
+                                      in_=x_tiles["xg"][:, g].rearrange("p r u -> p (r u)").bitcast(BF16))
+
+        def tables():
+            fcv = fc[:].rearrange("p m (i c) -> p m i c", c=2)
+            c2v = cos2[:].rearrange("p m (i c) -> p m i c", c=2)
+            s2v = sin2[:].rearrange("p m (i c) -> p m i c", c=2)
+            for dst, c, sign in ((c2v[:, :, :, 0:1], 0, 1.0), (c2v[:, :, :, 1:2], 0, 1.0),
+                                 (s2v[:, :, :, 1:2], 1, 1.0), (s2v[:, :, :, 0:1], 1, -1.0)):
+                nc.gpsimd.tensor_scalar(out=dst, in0=fcv[:, :, :, c:c + 1], scalar1=sign, scalar2=0.0,
+                                        op0=MULT, op1=ADD)
+
+        late = {}
+        staged = {}
+
+        def stage_tile(q, m):
+            if (q, m) not in staged:
+                ost = late["ost"].tile([P, 4, HD], F32, name="ost", tag="ost")
+                staged[(q, m)] = ost
+            return staged[(q, m)]
+
+        def rope_mul(q, m):
+            bank = acc[(q, ROPE, m)]
+            t1 = late["tmp"].tile([P, 512], F32, name="t1", tag="t1")
+            t2 = late["tmp"].tile([P, 512], F32, name="t2", tag="t2")
+            nc.vector.tensor_tensor(out=t1[:].rearrange("p (h j) -> p h j", h=4),
+                                    in0=bank[:].rearrange("p (h j) -> p h j", h=4),
+                                    in1=cos2[:, m:m + 1, :].to_broadcast([P, 4, P]), op=MULT)
+            nc.vector.tensor_tensor(
+                out=t2[:].rearrange("p (h i e) -> p h i e", h=4, e=2),
+                in0=bank[:].rearrange("p (h i e) -> p h i e", h=4, e=2)[:, :, :, ::-1],
+                in1=sin2[:, m:m + 1, :].rearrange("p o (i e) -> p o i e", e=2).to_broadcast([P, 4, P // 2, 2]),
+                op=MULT)
+            return t1, t2
+
+        def rope_add(q, m, t1, t2):
+            ost = stage_tile(q, m)
+            eng = nc.gpsimd if m < GPSIMD_ADDS else nc.vector
+            eng.tensor_tensor(out=ost[:, :, P:HD], in0=t1[:].rearrange("p (h j) -> p h j", h=4),
+                              in1=t2[:].rearrange("p (h j) -> p h j", h=4), op=ADD)
+
+        def store(q, m, lo, hi):
+            nc.sync.dma_start(out=out_view[m][:, 4 * q:4 * (q + 1), lo:hi], in_=staged[(q, m)][:, :, lo:hi])
+
+        def evac_rope(q):
+            last = q == QUADS - 1
+            prods = {}
+            for m in range(MT + 1):
+                if m < MT:
+                    prods[m] = rope_mul(q, m)
+                if last and m in WOVEN:
+                    quantize(WOVEN[m], NOPE)
+                    multiply(WOVEN[m], NOPE)
+                if m >= 1:
+                    t1, t2 = prods[m - 1]
+                    rope_add(q, m - 1, t1, t2)
+                    if last:
+                        store(q, m - 1, P, HD)
+
+        def evac_nope(q):
+            last = q == QUADS - 1
+            for m in range(MT):
+                ost = stage_tile(q, m)
+                src = acc[(q, NOPE, m)][:].rearrange("p (h f) -> p h f", h=4)
+                if last and m % 2 == 1:
+                    nc.vector.tensor_copy(out=ost[:, :, 0:P], in_=src)
+                else:
+                    nc.scalar.copy(out=ost[:, :, 0:P], in_=src)
+                if last:
+                    store(q, m, 0, P)
+                else:
+                    store(q, m, 0, HD)
+
+        blocks = []
+        for n in range(UNITS - G):
+            blocks.append((n, ROPE))
+            blocks.append((n, NOPE))
+        for s in (ROPE, NOPE):
+            for n in range(UNITS - G, UNITS):
+                blocks.append((n, s))
+        nb = len(blocks)
+        state = {"widened": 0}
+        waiting = []
+
+        def step(j):
+            if j < nb:
+                n, s = blocks[j]
+                while state["widened"] < min(UNITS, n + LEAD + 1):
+                    widen(state["widened"])
+                    state["widened"] += 1
+            if j + S_LEAD < nb and blocks[j + S_LEAD] in SCALAR_BLOCKS:
+                n, s = blocks[j + S_LEAD]
+                interleave(n, s)
+            if j < nb and blocks[j] not in SCALAR_BLOCKS:
+                n, s = blocks[j]
+                interleave(n, s)
+            if 1 <= j <= nb and not (blocks[j - 1][1] == NOPE and blocks[j - 1][0] in WOVEN_UNITS):
+                n, s = blocks[j - 1]
+                quantize(n, s)
+                waiting.append((n, s))
+            if j == TABLE_STEP:
+                tables()
+            for m in range(MT):
+                if X_STEP[m] == j:
+                    x_turn(m)
+            if j == max(X_STEP):
+                x_quantize()
+            if j >= max(X_STEP):
+                for n, s in waiting:
+                    multiply(n, s)
+                waiting.clear()
+            if 2 <= j <= nb + 1:
+                n, s = blocks[j - 2]
+                if n % G == G - 1:
+                    if s == ROPE:
+                        evac_rope(n // G)
+                    else:
+                        evac_nope(n // G)
+
+        with tc.tile_pool(name="xstage", bufs=1) as xp:
+            xg = xp.tile([P, G, T, 2], F32, name="xg", align_bytes=64)
+            x_tiles["xg"] = xg
+            for what, idx in (("w", 0), ("w", 1), ("w", 2), ("x", 0), ("x", 1), ("x", 2), ("w", 3), ("x", 3), ("f", 0)):
+                if what == "w":
+                    load_w(idx)
+                elif what == "f":
+                    nc.sync.dma_start(out=fc[:], in_=freq_cis.rearrange("(m p) i c -> p m (i c)", p=P))
+                else:
+                    x_sb = xp.tile([P, K], BF16, name="x_sb", tag="x_sb", bufs=MT)
+                    x_tiles[idx] = x_sb
+                    nc.sync.dma_start(out=x_sb[:], in_=x_view[idx])
+            for n in range(4, UNITS):
+                load_w(n)
+            for j in range(max(X_STEP) + 1):
+                step(j)
+
+        late["ost"] = ctx.enter_context(tc.tile_pool(name="ost", bufs=8))
+        late["tmp"] = ctx.enter_context(tc.tile_pool(name="tmp", bufs=4))
+        for j in range(max(X_STEP) + 1, nb + 2):
+            step(j)

@@ -25,7 +25,7 @@ UNITS = QUADS * G
 NOPE, ROPE = 0, 1
 LEAD = 3
 S_LEAD = 2
-GPSIMD_ADDS = 3
+GPSIMD_ADDS = 4
 X_STEP = (2, 2, 3, 3)
 TABLE_STEP = 3
 VECTOR_PLANES = ((0, 2), (0, 3), (1, 2), (1, 3))

@@ -29,7 +29,7 @@ GPSIMD_ADDS = 4
 X_STEP = (2, 2, 3, 3)
 TABLE_STEP = 3
 VECTOR_PLANES = ((0, 2), (0, 3), (1, 2), (1, 3))
-SCALAR_BLOCKS = ((9, NOPE), (12, NOPE), (13, NOPE), (14, NOPE), (15, NOPE))
+SCALAR_BLOCKS = ((12, NOPE), (13, NOPE), (14, NOPE), (15, NOPE))
 
 WOVEN_UNITS = (13, 14)
 WOVEN = {1: 13, 3: 14}

@@ -97,8 +97,8 @@ def tile_multiheadlatentattention_pb_kernel(tc, x, freq_cis, Wq_bytes, Wq_scale,
         def interleave(n, s):
             gr = gr_pool.tile([P, 2048], BF16, name="gr", tag="gr", align_bytes=64)
             grouped[(n, s)] = gr
-            dst = gr[:].rearrange("p (h a i t) -> p h a t i", h=4, i=4, t=4)
-            src = planes[n][:].rearrange("p t (h s a i) -> p s h a t i", s=2, a=32, i=4)[:, s]
+            dst = gr[:].rearrange("p (h a i t) -> p h a t i", h=4, i=8, t=4)
+            src = planes[n][:].rearrange("p t (h s a i) -> p s h a t i", s=2, a=16, i=8)[:, s]
             if (n, s) in SCALAR_BLOCKS:
                 nc.scalar.copy(out=dst, in_=src)
             else:

@@ -151,7 +151,7 @@ def tile_multiheadlatentattention_pb_kernel(tc, x, freq_cis, Wq_bytes, Wq_scale,
             c2v = cos2[:].rearrange("p m (i c) -> p m i c", c=2)
             s2v = sin2[:].rearrange("p m (i c) -> p m i c", c=2)
             for dst, c, sign in ((c2v[:, :, :, 0:1], 0, 1.0), (c2v[:, :, :, 1:2], 0, 1.0),
-                                 (s2v[:, :, :, 1:2], 1, 1.0), (s2v[:, :, :, 0:1], 1, -1.0)):
+                                 (s2v[:, :, :, 0:1], 1, 1.0), (s2v[:, :, :, 1:2], 1, -1.0)):
                 nc.gpsimd.tensor_scalar(out=dst, in0=fcv[:, :, :, c:c + 1], scalar1=sign, scalar2=0.0,
                                         op0=MULT, op1=ADD)
 
@@ -171,18 +171,17 @@ def tile_multiheadlatentattention_pb_kernel(tc, x, freq_cis, Wq_bytes, Wq_scale,
             nc.vector.tensor_tensor(out=t1[:].rearrange("p (h j) -> p h j", h=4),
                                     in0=bank[:].rearrange("p (h j) -> p h j", h=4),
                                     in1=cos2[:, m:m + 1, :].to_broadcast([P, 4, P]), op=MULT)
-            nc.vector.tensor_tensor(
-                out=t2[:].rearrange("p (h i e) -> p h i e", h=4, e=2),
-                in0=bank[:].rearrange("p (h i e) -> p h i e", h=4, e=2)[:, :, :, ::-1],
-                in1=sin2[:, m:m + 1, :].rearrange("p o (i e) -> p o i e", e=2).to_broadcast([P, 4, P // 2, 2]),
-                op=MULT)
+            nc.vector.tensor_tensor(out=t2[:].rearrange("p (h j) -> p h j", h=4),
+                                    in0=bank[:].rearrange("p (h j) -> p h j", h=4),
+                                    in1=sin2[:, m:m + 1, :].to_broadcast([P, 4, P]), op=MULT)
             return t1, t2
 
         def rope_add(q, m, t1, t2):
             ost = stage_tile(q, m)
             eng = nc.gpsimd if m < GPSIMD_ADDS else nc.vector
-            eng.tensor_tensor(out=ost[:, :, P:HD], in0=t1[:].rearrange("p (h j) -> p h j", h=4),
-                              in1=t2[:].rearrange("p (h j) -> p h j", h=4), op=ADD)
+            eng.tensor_tensor(out=ost[:, :, P:HD].rearrange("p h (i e) -> p h i e", e=2),
+                              in0=t1[:].rearrange("p (h i e) -> p h i e", h=4, e=2),
+                              in1=t2[:].rearrange("p (h i e) -> p h i e", h=4, e=2)[:, :, :, ::-1], op=ADD)
 
         def store(q, m, lo, hi):
             nc.sync.dma_start(out=out_view[m][:, 4 * q:4 * (q + 1), lo:hi], in_=staged[(q, m)][:, :, lo:hi])

@@ -25,14 +25,13 @@ UNITS = QUADS * G
 NOPE, ROPE = 0, 1
 LEAD = 3
 S_LEAD = 2
-GPSIMD_ADDS = 4
 X_STEP = (2, 2, 3, 3)
 TABLE_STEP = 3
 VECTOR_PLANES = ((0, 2), (0, 3), (1, 2), (1, 3))
 SCALAR_BLOCKS = ((12, NOPE), (13, NOPE), (14, NOPE), (15, NOPE))
 
-WOVEN_UNITS = (13, 14)
-WOVEN = {1: 13, 3: 14}
+WOVEN_UNITS = (13, 14, 15)
+WOVEN = {1: 13, 2: 14, 3: 15}
 
 FLOPS = 2 * T * K * HEADS * HD
 
@@ -178,7 +177,7 @@ def tile_multiheadlatentattention_pb_kernel(tc, x, freq_cis, Wq_bytes, Wq_scale,
 
         def rope_add(q, m, t1, t2):
             ost = stage_tile(q, m)
-            eng = nc.gpsimd if m < GPSIMD_ADDS else nc.vector
+            eng = nc.vector if (q == QUADS - 1 and m == MT - 1) else nc.gpsimd
             eng.tensor_tensor(out=ost[:, :, P:HD].rearrange("p h (i e) -> p h i e", e=2),
                               in0=t1[:].rearrange("p (h i e) -> p h i e", h=4, e=2),
                               in1=t2[:].rearrange("p (h i e) -> p h i e", h=4, e=2)[:, :, :, ::-1], op=ADD)

@@ -45,10 +45,10 @@ def tile_multiheadlatentattention_pb_kernel(tc, x, freq_cis, Wq_bytes, Wq_scale,
     with ExitStack() as ctx:
         ctx.enter_context(tc.manual_schedule())
         const = ctx.enter_context(tc.tile_pool(name="const", bufs=1))
-        wb_pool = ctx.enter_context(tc.tile_pool(name="wbytes", bufs=UNITS))
-        pl_pool = ctx.enter_context(tc.tile_pool(name="planes", bufs=6))
+        wb_pool = ctx.enter_context(tc.tile_pool(name="wbytes", bufs=12))
+        pl_pool = ctx.enter_context(tc.tile_pool(name="planes", bufs=7))
         gr_pool = ctx.enter_context(tc.tile_pool(name="grouped", bufs=7))
-        wc_pool = ctx.enter_context(tc.tile_pool(name="wcodes", bufs=10))
+        wc_pool = ctx.enter_context(tc.tile_pool(name="wcodes", bufs=14))
         psum = ctx.enter_context(tc.psum_pool(name="psum", bufs=8))
 
         wsc = const.tile([P, G, 4], F32, name="wsc")

@@ -22,17 +22,13 @@ G = K // 512
 MT = T // P
 QUADS = 4
 UNITS = QUADS * G
+LAST = UNITS - G
 NOPE, ROPE = 0, 1
-LEAD = 3
-S_LEAD = 2
-X_STEP = (2, 2, 3, 3)
-TABLE_STEP = 3
 VECTOR_PLANES = ((0, 2), (0, 3), (1, 2), (1, 3))
-SCALAR_BLOCKS = ((12, NOPE), (13, NOPE), (14, NOPE), (15, NOPE))
-
-WOVEN_UNITS = (13, 14, 15)
-WOVEN = {1: 13, 2: 14, 3: 15}
-
+NV = 2
+S_EARLY = (7, 11)
+S_LAG = 1
+PARTS = 1
 FLOPS = 2 * T * K * HEADS * HD
 
 
@@ -47,8 +43,10 @@ def tile_multiheadlatentattention_pb_kernel(tc, x, freq_cis, Wq_bytes, Wq_scale,
         const = ctx.enter_context(tc.tile_pool(name="const", bufs=1))
         wb_pool = ctx.enter_context(tc.tile_pool(name="wbytes", bufs=12))
         pl_pool = ctx.enter_context(tc.tile_pool(name="planes", bufs=7))
-        gr_pool = ctx.enter_context(tc.tile_pool(name="grouped", bufs=7))
+        gr_pool = ctx.enter_context(tc.tile_pool(name="grouped", bufs=4))
         wc_pool = ctx.enter_context(tc.tile_pool(name="wcodes", bufs=14))
+        ost_pool = ctx.enter_context(tc.tile_pool(name="ost", bufs=8))
+        tmp_pool = ctx.enter_context(tc.tile_pool(name="tmp", bufs=4))
         psum = ctx.enter_context(tc.psum_pool(name="psum", bufs=8))
 
         wsc = const.tile([P, G, 4], F32, name="wsc")
@@ -77,73 +75,107 @@ def tile_multiheadlatentattention_pb_kernel(tc, x, freq_cis, Wq_bytes, Wq_scale,
             else:
                 nc.sync.dma_start(out=wb[:], in_=w_view[g, :, :, cols])
 
+        x_tiles = {}
+
+        def load_x(m):
+            x_sb = ost_pool.tile([P, K], BF16, name="x_sb", tag="ost", align_bytes=64)
+            x_tiles[m] = x_sb
+            nc.sync.dma_start(out=x_sb[:], in_=x_view[m])
+
+        for what, idx in (("w", 0), ("w", 1), ("w", 2), ("x", 0), ("x", 1), ("x", 2), ("w", 3), ("x", 3), ("f", 0)):
+            if what == "w":
+                load_w(idx)
+            elif what == "f":
+                nc.sync.dma_start(out=fc[:], in_=freq_cis.rearrange("(m p) i c -> p m (i c)", p=P))
+            else:
+                load_x(idx)
+        for n in range(4, UNITS):
+            load_w(n)
+        xg = {}
+        for g in range(G):
+            xgt = ost_pool.tile([P, T, 2], F32, name="xg", tag="ost", align_bytes=64)
+            xg[g] = xgt
+
         planes = {}
 
-        def widen(n):
+        def plane_tile(n):
+            if n not in planes:
+                pl = pl_pool.tile([P, 4, 1024], BF16, name="pl", tag="pl", align_bytes=64)
+                planes[n] = pl
+            return planes[n]
+
+        def widen(n, on_vector):
             q, g = divmod(n, G)
-            pl = pl_pool.tile([P, 4, 1024], BF16, name="pl", tag="pl")
-            planes[n] = pl
             for t in range(4):
-                src = wbytes[n][:, t, :].bitcast(FP8)
-                if (n, t) in VECTOR_PLANES:
-                    nc.vector.tensor_scalar(out=pl[:, t, :], in0=src, scalar1=wsc[:, g, t:t + 1],
-                                            scalar2=None, op0=MULT)
-                else:
-                    nc.scalar.activation(out=pl[:, t, :], in_=src, func=COPY, scale=wsc[:, g, t:t + 1])
+                if ((n, t) in VECTOR_PLANES) == on_vector:
+                    pl = plane_tile(n)
+                    src = wbytes[n][:, t, :].bitcast(FP8)
+                    if on_vector:
+                        nc.vector.tensor_scalar(out=pl[:, t, :], in0=src, scalar1=wsc[:, g, t:t + 1],
+                                                scalar2=None, op0=MULT)
+                    else:
+                        nc.scalar.activation(out=pl[:, t, :], in_=src, func=COPY, scale=wsc[:, g, t:t + 1])
 
         grouped = {}
 
-        def interleave(n, s):
-            gr = gr_pool.tile([P, 2048], BF16, name="gr", tag="gr", align_bytes=64)
-            grouped[(n, s)] = gr
-            dst = gr[:].rearrange("p (h a i t) -> p h a t i", h=4, i=8, t=4)
-            src = planes[n][:].rearrange("p t (h s a i) -> p s h a t i", s=2, a=16, i=8)[:, s]
-            if (n, s) in SCALAR_BLOCKS:
-                nc.scalar.copy(out=dst, in_=src)
-            else:
+        def interleave(n, s, part, eng):
+            hs = slice(0, 4) if part is None else slice(part * 4 // PARTS, (part + 1) * 4 // PARTS)
+            nh = hs.stop - hs.start
+            gr = gr_pool.tile([P, 512 * nh], BF16, name="gr", tag="gr", bufs=7, align_bytes=64)
+            grouped[(n, s, part)] = gr
+            dst = gr[:].rearrange("p (h a i t) -> p h a t i", h=nh, i=8, t=4)
+            src = planes[n][:].rearrange("p t (h s a i) -> p s h a t i", s=2, a=16, i=8)[:, s, hs]
+            if eng == "v":
                 nc.vector.tensor_copy(out=dst, in_=src)
+            else:
+                nc.scalar.copy(out=dst, in_=src)
 
         codes = {}
 
-        def quantize(n, s):
-            wc = wc_pool.tile([P, 512], U32, name="wc", tag="wc", align_bytes=64)
-            ws = wc_pool.tile([P, 512], U8, name="ws", tag="ws", align_bytes=64)
-            codes[(n, s)] = (wc, ws)
-            nc.vector.quantize_mx(out=wc[:].bitcast(FP8X4), scales=ws[:], in_=grouped[(n, s)][:])
+        def quantize(n, s, part):
+            gr = grouped[(n, s, part)]
+            width = 512 if part is None else 512 // PARTS
+            wc = wc_pool.tile([P, width], U32, name="wc", tag="wc", align_bytes=64)
+            ws = wc_pool.tile([P, width], U8, name="ws", tag="ws", align_bytes=64)
+            codes[(n, s, part)] = (wc, ws, width)
+            nc.vector.quantize_mx(out=wc[:].bitcast(FP8X4), scales=ws[:], in_=gr[:])
 
         acc = {}
 
-        def multiply(n, s):
+        def multiply(n, s, part, ms=range(MT)):
             q, g = divmod(n, G)
-            wc, ws = codes[(n, s)]
-            for m in range(MT):
-                if g == 0:
+            wc, ws, width = codes[(n, s, part)]
+            for m in ms:
+                if g == 0 and not part:
                     bank = psum.tile([P, 512], F32, name="bank", tag="bank")
                     acc[(q, s, m)] = bank
+                cols = slice(0, 512) if part is None else slice(width * part, width * (part + 1))
                 toks = slice(P * m, P * (m + 1))
-                nc.tensor.matmul_mx(out=acc[(q, s, m)][:],
+                nc.tensor.matmul_mx(out=acc[(q, s, m)][:, cols],
                                     lhsT=xc[:, g, toks].bitcast(FP8X4), lhsT_scale=xs[:, g, toks],
                                     rhs=wc[:].bitcast(FP8X4), rhs_scale=ws[:],
                                     start=(g == 0), stop=(g == G - 1))
 
-        x_tiles = {}
+        turned = {}
 
-        def x_turn(m):
-            words = x_tiles[m][:].bitcast(F32)
-            for gp in range(G // 2):
+        def x_turn(mp):
+            for g in range(G):
                 xt = psum.tile([P, 2, 2, P], F32, name="xt", tag="bank")
-                for gg in range(2):
-                    g = 2 * gp + gg
+                turned[(mp, g)] = xt
+                for mm in range(2):
+                    words = x_tiles[2 * mp + mm][:].bitcast(F32)
                     for u in range(2):
-                        nc.tensor.transpose(out=xt[:, gg, u, :], in_=words[:, 256 * g + u:256 * (g + 1):2],
+                        nc.tensor.transpose(out=xt[:, mm, u, :], in_=words[:, 256 * g + u:256 * (g + 1):2],
                                             identity=ident[:])
-                nc.vector.tensor_copy(out=x_tiles["xg"][:, 2 * gp:2 * gp + 2, P * m:P * (m + 1), :],
-                                      in_=xt[:].rearrange("p g u r -> p g r u"))
+
+        def x_out(mp, g):
+            nc.vector.tensor_copy(out=xg[g][:, 2 * P * mp:2 * P * (mp + 1), :].rearrange("p (m r) u -> p m r u", m=2),
+                                  in_=turned[(mp, g)][:].rearrange("p m u r -> p m r u"))
 
         def x_quantize():
             for g in range(G):
                 nc.vector.quantize_mx(out=xc[:, g, :].bitcast(FP8X4), scales=xs[:, g, :],
-                                      in_=x_tiles["xg"][:, g].rearrange("p r u -> p (r u)").bitcast(BF16))
+                                      in_=xg[g][:].rearrange("p r u -> p (r u)").bitcast(BF16))
 
         def tables():
             fcv = fc[:].rearrange("p m (i c) -> p m i c", c=2)
@@ -154,130 +186,178 @@ def tile_multiheadlatentattention_pb_kernel(tc, x, freq_cis, Wq_bytes, Wq_scale,
                 nc.gpsimd.tensor_scalar(out=dst, in0=fcv[:, :, :, c:c + 1], scalar1=sign, scalar2=0.0,
                                         op0=MULT, op1=ADD)
 
-        late = {}
         staged = {}
 
         def stage_tile(q, m):
             if (q, m) not in staged:
-                ost = late["ost"].tile([P, 4, HD], F32, name="ost", tag="ost")
+                ost = ost_pool.tile([P, 4, HD], F32, name="ost", tag="ost", align_bytes=64)
                 staged[(q, m)] = ost
             return staged[(q, m)]
 
+        prods = {}
+
         def rope_mul(q, m):
             bank = acc[(q, ROPE, m)]
-            t1 = late["tmp"].tile([P, 512], F32, name="t1", tag="t1")
-            t2 = late["tmp"].tile([P, 512], F32, name="t2", tag="t2")
-            nc.vector.tensor_tensor(out=t1[:].rearrange("p (h j) -> p h j", h=4),
-                                    in0=bank[:].rearrange("p (h j) -> p h j", h=4),
-                                    in1=cos2[:, m:m + 1, :].to_broadcast([P, 4, P]), op=MULT)
-            nc.vector.tensor_tensor(out=t2[:].rearrange("p (h j) -> p h j", h=4),
-                                    in0=bank[:].rearrange("p (h j) -> p h j", h=4),
-                                    in1=sin2[:, m:m + 1, :].to_broadcast([P, 4, P]), op=MULT)
-            return t1, t2
+            t1 = tmp_pool.tile([P, 512], F32, name="t1", tag="t1")
+            t2 = tmp_pool.tile([P, 512], F32, name="t2", tag="t2")
+            for dst, table in ((t1, cos2), (t2, sin2)):
+                nc.vector.tensor_tensor(out=dst[:].rearrange("p (h j) -> p h j", h=4),
+                                        in0=bank[:].rearrange("p (h j) -> p h j", h=4),
+                                        in1=table[:, m:m + 1, :].to_broadcast([P, 4, P]), op=MULT)
+            prods[(q, m)] = (t1, t2)
 
-        def rope_add(q, m, t1, t2):
+        def rope_add(q, m, eng="g"):
+            t1, t2 = prods[(q, m)]
             ost = stage_tile(q, m)
-            eng = nc.vector if (q == QUADS - 1 and m == MT - 1) else nc.gpsimd
-            eng.tensor_tensor(out=ost[:, :, P:HD].rearrange("p h (i e) -> p h i e", e=2),
-                              in0=t1[:].rearrange("p (h i e) -> p h i e", h=4, e=2),
-                              in1=t2[:].rearrange("p (h i e) -> p h i e", h=4, e=2)[:, :, :, ::-1], op=ADD)
+            (nc.vector if eng == "v" else nc.gpsimd).tensor_tensor(
+                out=ost[:, :, P:HD].rearrange("p h (i e) -> p h i e", e=2),
+                in0=t1[:].rearrange("p (h i e) -> p h i e", h=4, e=2),
+                in1=t2[:].rearrange("p (h i e) -> p h i e", h=4, e=2)[:, :, :, ::-1], op=ADD)
 
-        def store(q, m, lo, hi):
-            nc.sync.dma_start(out=out_view[m][:, 4 * q:4 * (q + 1), lo:hi], in_=staged[(q, m)][:, :, lo:hi])
+        def heads_of(part):
+            return slice(0, 4) if part is None else slice(part * 4 // PARTS, (part + 1) * 4 // PARTS)
 
-        def evac_rope(q):
-            last = q == QUADS - 1
-            prods = {}
-            for m in range(MT + 1):
-                if m < MT:
-                    prods[m] = rope_mul(q, m)
-                if last and m in WOVEN:
-                    quantize(WOVEN[m], NOPE)
-                    multiply(WOVEN[m], NOPE)
-                if m >= 1:
-                    t1, t2 = prods[m - 1]
-                    rope_add(q, m - 1, t1, t2)
-                    if last:
-                        store(q, m - 1, P, HD)
+        def store(q, m, lo, hi, part):
+            hs = heads_of(part)
+            nc.sync.dma_start(out=out_view[m][:, 4 * q + hs.start:4 * q + hs.stop, lo:hi],
+                              in_=staged[(q, m)][:, hs, lo:hi])
 
-        def evac_nope(q):
-            last = q == QUADS - 1
+        def nope_copy(q, m, part, eng):
+            ost = stage_tile(q, m)
+            hs = heads_of(part)
+            src = acc[(q, NOPE, m)][:].rearrange("p (h f) -> p h f", h=4)[:, hs]
+            if eng == "v":
+                nc.vector.tensor_copy(out=ost[:, hs, 0:P], in_=src)
+            else:
+                nc.scalar.copy(out=ost[:, hs, 0:P], in_=src)
+
+        progs = {"s": [], "t": [], "v": [], "g": [], "d": []}
+
+        def put(eng, gives, needs, fn, *args):
+            progs[eng].append((gives, needs, fn, args))
+
+        def on_v(n):
+            return any(v[0] == n for v in VECTOR_PLANES)
+
+        def W(n):
+            put("s", ("ws", n), [], widen, n, False)
+
+        def WV(n):
+            if on_v(n):
+                put("v", ("wv", n), [], widen, n, True)
+
+        def I(n, s, part=None, eng="v"):
+            put(eng, ("gr", n, s, part), [("ws", n)] + ([("wv", n)] if on_v(n) else []), interleave, n, s, part, eng)
+
+        def Q(n, s, part=None):
+            put("v", ("q", n, s, part), [("gr", n, s, part)], quantize, n, s, part)
+
+        def M(n, s, part=None):
+            put("t", ("m", n, s, part), [("q", n, s, part), ("xq",)], multiply, n, s, part)
+
+        def NC(q, m, part=None, eng="s"):
+            put(eng, ("nc", q, m, part), [("m", G * q + G - 1, NOPE, part)], nope_copy, q, m, part, eng)
+
+        def XT(mp):
+            put("t", ("xt", mp), [], x_turn, mp)
+
+        def XO(mp, gs=range(G)):
+            for g in gs:
+                put("v", ("xo", mp, g), [("xt", mp)], x_out, mp, g)
+
+        def XQ():
+            put("v", ("xq",), [("xo", mp, g) for mp in range(2) for g in range(G)], x_quantize)
+
+        def RM(q, m):
+            put("v", ("rm", q, m), [("m", G * q + G - 1, ROPE, None), ("tab",)], rope_mul, q, m)
+
+        def RA(q, m, eng="g"):
+            put(eng, ("ra", q, m), [("rm", q, m)], rope_add, q, m, eng)
+
+        def ST(q, m, lo, hi, part=None):
+            put("d", ("st", q, m, lo, part), ([("nc", q, m, part)] if lo == 0 else []) + ([("ra", q, m)] if hi == HD else []),
+                store, q, m, lo, hi, part)
+
+        last_parts = range(PARTS) if PARTS > 1 else (None,)
+        for n in range(UNITS):
+            W(n)
+            q, g = divmod(n, G)
+            if n - S_LAG in S_EARLY:
+                I(n - S_LAG, NOPE, None, "s")
+            if g == G - 1 and q >= 1:
+                for m in range(NV):
+                    NC(q - 1, m)
+        for n in range(LAST, UNITS):
+            I(n, NOPE, None, "s")
+        for n in range(UNITS):
+            if n < 2:
+                WV(n)
+        order = [(n, s) for n in range(LAST) for s in (NOPE, ROPE)] + [(n, ROPE) for n in range(LAST, UNITS)]
+        for j in range(len(order) + 1):
+            if j < len(order) and not (order[j][1] == NOPE and order[j][0] in S_EARLY):
+                I(*order[j])
+            if j % 2 == 0 and 2 + j // 2 < UNITS:
+                WV(2 + j // 2)
+            if j >= 1:
+                Q(*order[j - 1])
+            if j == 2:
+                XO(0)
+            if j == 3:
+                XO(1)
+                XQ()
+            if j >= 2 and order[j - 2][1] == ROPE and order[j - 2][0] % G == G - 1 and j - 2 < len(order) - 1:
+                for m in range(MT):
+                    RM(order[j - 2][0] // G, m)
+                for m in range(NV, MT):
+                    NC(order[j - 2][0] // G, m, None, "v")
+        Q(LAST, NOPE, last_parts[0])
+        RM(3, 0)
+        RM(3, 1)
+        Q(13, NOPE, last_parts[0])
+        RM(3, 2)
+        Q(14, NOPE, last_parts[0])
+        RM(3, 3)
+        Q(15, NOPE, last_parts[0])
+        RA(3, 3, "v")
+        for part in last_parts[1:]:
+            for n in range(LAST, UNITS):
+                Q(n, NOPE, part)
+        for part in last_parts:
             for m in range(MT):
-                ost = stage_tile(q, m)
-                src = acc[(q, NOPE, m)][:].rearrange("p (h f) -> p h f", h=4)
-                if last and m % 2 == 1:
-                    nc.vector.tensor_copy(out=ost[:, :, 0:P], in_=src)
-                else:
-                    nc.scalar.copy(out=ost[:, :, 0:P], in_=src)
-                if last:
-                    store(q, m, 0, P)
-                else:
-                    store(q, m, 0, HD)
-
-        blocks = []
-        for n in range(UNITS - G):
-            blocks.append((n, ROPE))
-            blocks.append((n, NOPE))
-        for s in (ROPE, NOPE):
-            for n in range(UNITS - G, UNITS):
-                blocks.append((n, s))
-        nb = len(blocks)
-        state = {"widened": 0}
-        waiting = []
-
-        def step(j):
-            if j < nb:
-                n, s = blocks[j]
-                while state["widened"] < min(UNITS, n + LEAD + 1):
-                    widen(state["widened"])
-                    state["widened"] += 1
-            if j + S_LEAD < nb and blocks[j + S_LEAD] in SCALAR_BLOCKS:
-                n, s = blocks[j + S_LEAD]
-                interleave(n, s)
-            if j < nb and blocks[j] not in SCALAR_BLOCKS:
-                n, s = blocks[j]
-                interleave(n, s)
-            if 1 <= j <= nb and not (blocks[j - 1][1] == NOPE and blocks[j - 1][0] in WOVEN_UNITS):
-                n, s = blocks[j - 1]
-                quantize(n, s)
-                waiting.append((n, s))
-            if j == TABLE_STEP:
-                tables()
+                NC(3, m, part, "v" if m % 2 else "s")
+        XT(0)
+        XT(1)
+        for n, s in order:
+            M(n, s)
+        for part in last_parts:
+            for n in range(LAST, UNITS):
+                M(n, NOPE, part)
+        put("g", ("tab",), [], tables)
+        for q in range(QUADS):
             for m in range(MT):
-                if X_STEP[m] == j:
-                    x_turn(m)
-            if j == max(X_STEP):
-                x_quantize()
-            if j >= max(X_STEP):
-                for n, s in waiting:
-                    multiply(n, s)
-                waiting.clear()
-            if 2 <= j <= nb + 1:
-                n, s = blocks[j - 2]
-                if n % G == G - 1:
-                    if s == ROPE:
-                        evac_rope(n // G)
-                    else:
-                        evac_nope(n // G)
+                if (q, m) != (3, 3):
+                    RA(q, m)
+        for q in range(QUADS - 1):
+            for m in range(MT):
+                ST(q, m, 0, HD)
+        for m in range(MT):
+            ST(3, m, P, HD)
+        for part in last_parts:
+            for m in (0, 1, 2, 3):
+                ST(3, m, 0, P, part)
 
-        with tc.tile_pool(name="xstage", bufs=1) as xp:
-            xg = xp.tile([P, G, T, 2], F32, name="xg", align_bytes=64)
-            x_tiles["xg"] = xg
-            for what, idx in (("w", 0), ("w", 1), ("w", 2), ("x", 0), ("x", 1), ("x", 2), ("w", 3), ("x", 3), ("f", 0)):
-                if what == "w":
-                    load_w(idx)
-                elif what == "f":
-                    nc.sync.dma_start(out=fc[:], in_=freq_cis.rearrange("(m p) i c -> p m (i c)", p=P))
-                else:
-                    x_sb = xp.tile([P, K], BF16, name="x_sb", tag="x_sb", bufs=MT)
-                    x_tiles[idx] = x_sb
-                    nc.sync.dma_start(out=x_sb[:], in_=x_view[idx])
-            for n in range(4, UNITS):
-                load_w(n)
-            for j in range(max(X_STEP) + 1):
-                step(j)
-
-        late["ost"] = ctx.enter_context(tc.tile_pool(name="ost", bufs=8))
-        late["tmp"] = ctx.enter_context(tc.tile_pool(name="tmp", bufs=4))
-        for j in range(max(X_STEP) + 1, nb + 2):
-            step(j)
+        done = set()
+        at = {e: 0 for e in progs}
+        moved = True
+        while moved:
+            moved = False
+            for e in ("s", "v", "t", "g", "d"):
+                while at[e] < len(progs[e]):
+                    gives, needs, fn, args = progs[e][at[e]]
+                    if not all(k in done for k in needs):
+                        break
+                    fn(*args)
+                    done.add(gives)
+                    at[e] += 1
+                    moved = True
+        assert all(at[e] == len(progs[e]) for e in progs)

@@ -24,11 +24,10 @@ QUADS = 4
 UNITS = QUADS * G
 LAST = UNITS - G
 NOPE, ROPE = 0, 1
-VECTOR_PLANES = ((0, 2), (0, 3), (1, 2), (1, 3))
-NV = 2
-S_EARLY = (7, 11)
-S_LAG = 1
-PARTS = 1
+PE_BLOCKS = (1, 2, 3, 5, 6, 7, 9, 10, 11, 12, 13, 14)
+VP = tuple(range(2, 12))
+VECTOR_PLANES = ((0, 2), (0, 3), (1, 2), (1, 3)) + tuple((n, 3) for n in VP)
+LAST_NOPE = (12, 13, 15, 14)
 FLOPS = 2 * T * K * HEADS * HD
 
 
@@ -41,13 +40,13 @@ def tile_multiheadlatentattention_pb_kernel(tc, x, freq_cis, Wq_bytes, Wq_scale,
     with ExitStack() as ctx:
         ctx.enter_context(tc.manual_schedule())
         const = ctx.enter_context(tc.tile_pool(name="const", bufs=1))
-        wb_pool = ctx.enter_context(tc.tile_pool(name="wbytes", bufs=12))
+        wb_pool = ctx.enter_context(tc.tile_pool(name="wbytes", bufs=11))
         pl_pool = ctx.enter_context(tc.tile_pool(name="planes", bufs=7))
         gr_pool = ctx.enter_context(tc.tile_pool(name="grouped", bufs=4))
-        wc_pool = ctx.enter_context(tc.tile_pool(name="wcodes", bufs=14))
+        wc_pool = ctx.enter_context(tc.tile_pool(name="wcodes", bufs=9))
         ost_pool = ctx.enter_context(tc.tile_pool(name="ost", bufs=8))
         tmp_pool = ctx.enter_context(tc.tile_pool(name="tmp", bufs=4))
-        psum = ctx.enter_context(tc.psum_pool(name="psum", bufs=8))
+        psum = ctx.enter_context(tc.psum_pool(name="psum", bufs=4))
 
         wsc = const.tile([P, G, 4], F32, name="wsc")
         nc.scalar.dma_start(out=wsc[:], in_=Wq_scale.rearrange("(g p t) o -> p g (t o)", p=P, t=4))
@@ -56,6 +55,8 @@ def tile_multiheadlatentattention_pb_kernel(tc, x, freq_cis, Wq_bytes, Wq_scale,
         nc.scalar.activation(out=warm[:, 1:2], in_=warm[:, 0:1], func=COPY)
         ident = const.tile([P, P], F32, name="ident")
         make_identity(nc, ident[:])
+        ident_bf = const.tile([P, P], BF16, name="ident_bf")
+        make_identity(nc, ident_bf[:])
         fc = const.tile([P, MT, P], BF16, name="fc")
         cos2 = const.tile([P, MT, P], F32, name="cos2")
         sin2 = const.tile([P, MT, P], F32, name="sin2")
@@ -69,7 +70,13 @@ def tile_multiheadlatentattention_pb_kernel(tc, x, freq_cis, Wq_bytes, Wq_scale,
             cols = slice(1024 * q, 1024 * (q + 1))
             wb = wb_pool.tile([P, 4, 1024], U8, name="wb", tag="wb")
             wbytes[n] = wb
-            if n == 0:
+            if n >= LAST:
+                rows = wb[:].rearrange("p t (s h f) -> p s t h f", s=2, h=4)
+                cols = w_view[g].rearrange("p t (q h s f) -> p q s t h f", q=QUADS, h=4, s=2)
+                for s in (ROPE, NOPE):
+                    for t in range(4):
+                        nc.sync.dma_start(out=rows[:, s, t], in_=cols[:, q, s, t])
+            elif n == 0:
                 for t in range(4):
                     nc.sync.dma_start(out=wb[:, t, :], in_=w_view[g, :, t, cols])
             else:
@@ -98,18 +105,19 @@ def tile_multiheadlatentattention_pb_kernel(tc, x, freq_cis, Wq_bytes, Wq_scale,
 
         planes = {}
 
-        def plane_tile(n):
-            if n not in planes:
-                pl = pl_pool.tile([P, 4, 1024], BF16, name="pl", tag="pl", align_bytes=64)
-                planes[n] = pl
-            return planes[n]
+        def plane_tile(n, half):
+            if (n, half) not in planes:
+                pl = pl_pool.tile([P, 4, 1024 if half is None else 512], BF16, name="pl", tag="pl", align_bytes=64)
+                planes[(n, half)] = pl
+            return planes[(n, half)]
 
-        def widen(n, on_vector):
+        def widen(n, on_vector, half=None):
             q, g = divmod(n, G)
+            part = slice(0, 1024) if half is None else slice(512 * half, 512 * (half + 1))
             for t in range(4):
                 if ((n, t) in VECTOR_PLANES) == on_vector:
-                    pl = plane_tile(n)
-                    src = wbytes[n][:, t, :].bitcast(FP8)
+                    pl = plane_tile(n, half)
+                    src = wbytes[n][:, t, part].bitcast(FP8)
                     if on_vector:
                         nc.vector.tensor_scalar(out=pl[:, t, :], in0=src, scalar1=wsc[:, g, t:t + 1],
                                                 scalar2=None, op0=MULT)
@@ -118,49 +126,83 @@ def tile_multiheadlatentattention_pb_kernel(tc, x, freq_cis, Wq_bytes, Wq_scale,
 
         grouped = {}
 
-        def interleave(n, s, part, eng):
-            hs = slice(0, 4) if part is None else slice(part * 4 // PARTS, (part + 1) * 4 // PARTS)
-            nh = hs.stop - hs.start
-            gr = gr_pool.tile([P, 512 * nh], BF16, name="gr", tag="gr", bufs=7, align_bytes=64)
-            grouped[(n, s, part)] = gr
-            dst = gr[:].rearrange("p (h a i t) -> p h a t i", h=nh, i=8, t=4)
-            src = planes[n][:].rearrange("p t (h s a i) -> p s h a t i", s=2, a=16, i=8)[:, s, hs]
+        def group_tile(n, s, made_by):
+            gr = gr_pool.tile([P, 2048], BF16, name="gr", tag="gr" + made_by, bufs=4, align_bytes=64)
+            grouped[(n, s)] = gr
+            return gr
+
+        def half_of(n, s):
+            if n < LAST:
+                return planes[(n, None)][:].rearrange("p t (h s a i) -> p s h a t i", s=2, a=16, i=8)[:, s]
+            return planes[(n, s)][:].rearrange("p t (h a i) -> p h a t i", a=16, i=8)
+
+        def interleave(n, s, eng="v"):
+            gr = group_tile(n, s, "v" if eng == "v" else "s")
+            dst = gr[:].rearrange("p (h a i t) -> p h a t i", h=4, i=8, t=4)
+            src = half_of(n, s)
             if eng == "v":
                 nc.vector.tensor_copy(out=dst, in_=src)
             else:
                 nc.scalar.copy(out=dst, in_=src)
 
+        woven = {}
+
+        def pe_interleave(n):
+            src = half_of(n, NOPE)
+            for b in range(2):
+                il = psum.tile([P, 1024], BF16, name="il", tag="il", bufs=2)
+                woven[(n, b)] = il
+                for hh in range(2):
+                    nc.tensor.matmul(out=il[:, 512 * hh:512 * (hh + 1)].rearrange("p (a i t) -> p a t i", i=8, t=4),
+                                     lhsT=ident_bf[:], rhs=src[:, 2 * b + hh], start=True, stop=True)
+
+        def pe_evacuate(n, eng="s"):
+            gr = group_tile(n, NOPE, eng)
+            for b in range(2):
+                dst = gr[:, 1024 * b:1024 * (b + 1)]
+                if eng == "v":
+                    nc.vector.tensor_copy(out=dst, in_=woven[(n, b)][:])
+                else:
+                    nc.scalar.copy(out=dst, in_=woven[(n, b)][:])
+
         codes = {}
 
-        def quantize(n, s, part):
-            gr = grouped[(n, s, part)]
-            width = 512 if part is None else 512 // PARTS
-            wc = wc_pool.tile([P, width], U32, name="wc", tag="wc", align_bytes=64)
-            ws = wc_pool.tile([P, width], U8, name="ws", tag="ws", align_bytes=64)
-            codes[(n, s, part)] = (wc, ws, width)
-            nc.vector.quantize_mx(out=wc[:].bitcast(FP8X4), scales=ws[:], in_=gr[:])
+        def quantize(n, s):
+            depth = 5 if s == ROPE else 7
+            wc = wc_pool.tile([P, 512], U32, name="wc", tag="wc%d" % s, bufs=depth, align_bytes=64)
+            ws = wc_pool.tile([P, 512], U8, name="ws", tag="ws%d" % s, bufs=depth, align_bytes=64)
+            codes[(n, s)] = (wc, ws)
+            nc.vector.quantize_mx(out=wc[:].bitcast(FP8X4), scales=ws[:], in_=grouped[(n, s)][:])
 
         acc = {}
 
-        def multiply(n, s, part, ms=range(MT)):
+        def one_pass(n, s, m):
             q, g = divmod(n, G)
-            wc, ws, width = codes[(n, s, part)]
+            rank = LAST_NOPE.index(n) if n >= LAST and s == NOPE else g
+            wc, ws = codes[(n, s)]
+            if rank == 0:
+                tag = "rope" if s == ROPE or (q == QUADS - 1 and m >= 2) else "nope"
+                bank = psum.tile([P, 512], F32, name="bank", tag=tag, bufs=4 if tag == "rope" else 2)
+                acc[(q, s, m)] = bank
+            toks = slice(P * m, P * (m + 1))
+            nc.tensor.matmul_mx(out=acc[(q, s, m)][:],
+                                lhsT=xc[:, g, toks].bitcast(FP8X4), lhsT_scale=xs[:, g, toks],
+                                rhs=wc[:].bitcast(FP8X4), rhs_scale=ws[:],
+                                start=(rank == 0), stop=(rank == G - 1))
+
+        def multiply(n, s, ms=range(MT)):
             for m in ms:
-                if g == 0 and not part:
-                    bank = psum.tile([P, 512], F32, name="bank", tag="bank")
-                    acc[(q, s, m)] = bank
-                cols = slice(0, 512) if part is None else slice(width * part, width * (part + 1))
-                toks = slice(P * m, P * (m + 1))
-                nc.tensor.matmul_mx(out=acc[(q, s, m)][:, cols],
-                                    lhsT=xc[:, g, toks].bitcast(FP8X4), lhsT_scale=xs[:, g, toks],
-                                    rhs=wc[:].bitcast(FP8X4), rhs_scale=ws[:],
-                                    start=(g == 0), stop=(g == G - 1))
+                one_pass(n, s, m)
+
+        def nope_passes(q, m):
+            for g in range(G):
+                one_pass(G * q + g, NOPE, m)
 
         turned = {}
 
         def x_turn(mp):
             for g in range(G):
-                xt = psum.tile([P, 2, 2, P], F32, name="xt", tag="bank")
+                xt = psum.tile([P, 2, 2, P], F32, name="xt", tag="rope", bufs=4)
                 turned[(mp, g)] = xt
                 for mm in range(2):
                     words = x_tiles[2 * mp + mm][:].bitcast(F32)
@@ -214,49 +256,64 @@ def tile_multiheadlatentattention_pb_kernel(tc, x, freq_cis, Wq_bytes, Wq_scale,
                 in0=t1[:].rearrange("p (h i e) -> p h i e", h=4, e=2),
                 in1=t2[:].rearrange("p (h i e) -> p h i e", h=4, e=2)[:, :, :, ::-1], op=ADD)
 
-        def heads_of(part):
-            return slice(0, 4) if part is None else slice(part * 4 // PARTS, (part + 1) * 4 // PARTS)
+        def store(q, m, lo, hi):
+            nc.sync.dma_start(out=out_view[m][:, 4 * q:4 * (q + 1), lo:hi], in_=staged[(q, m)][:, :, lo:hi])
 
-        def store(q, m, lo, hi, part):
-            hs = heads_of(part)
-            nc.sync.dma_start(out=out_view[m][:, 4 * q + hs.start:4 * q + hs.stop, lo:hi],
-                              in_=staged[(q, m)][:, hs, lo:hi])
-
-        def nope_copy(q, m, part, eng):
+        def nope_copy(q, m, eng="s"):
             ost = stage_tile(q, m)
-            hs = heads_of(part)
-            src = acc[(q, NOPE, m)][:].rearrange("p (h f) -> p h f", h=4)[:, hs]
+            src = acc[(q, NOPE, m)][:].rearrange("p (h f) -> p h f", h=4)
             if eng == "v":
-                nc.vector.tensor_copy(out=ost[:, hs, 0:P], in_=src)
+                nc.vector.tensor_copy(out=ost[:, :, 0:P], in_=src)
             else:
-                nc.scalar.copy(out=ost[:, hs, 0:P], in_=src)
+                nc.scalar.copy(out=ost[:, :, 0:P], in_=src)
 
         progs = {"s": [], "t": [], "v": [], "g": [], "d": []}
 
         def put(eng, gives, needs, fn, *args):
             progs[eng].append((gives, needs, fn, args))
 
-        def on_v(n):
-            return any(v[0] == n for v in VECTOR_PLANES)
-
         def W(n):
             put("s", ("ws", n), [], widen, n, False)
 
         def WV(n):
-            if on_v(n):
+            if n < LAST and any(v[0] == n for v in VECTOR_PLANES):
                 put("v", ("wv", n), [], widen, n, True)
 
-        def I(n, s, part=None, eng="v"):
-            put(eng, ("gr", n, s, part), [("ws", n)] + ([("wv", n)] if on_v(n) else []), interleave, n, s, part, eng)
+        def WH(n, s):
+            put("s", ("ws", n, s), [], widen, n, False, s)
 
-        def Q(n, s, part=None):
-            put("v", ("q", n, s, part), [("gr", n, s, part)], quantize, n, s, part)
+        def WVH(n, s):
+            if any(v[0] == n for v in VECTOR_PLANES):
+                put("v", ("wv", n, s), [], widen, n, True, s)
 
-        def M(n, s, part=None):
-            put("t", ("m", n, s, part), [("q", n, s, part), ("xq",)], multiply, n, s, part)
+        def wid(n, s):
+            if n >= LAST:
+                return [("ws", n, s)] + ([("wv", n, s)] if any(v[0] == n for v in VECTOR_PLANES) else [])
+            return [("ws", n)] + ([("wv", n)] if any(v[0] == n for v in VECTOR_PLANES) else [])
 
-        def NC(q, m, part=None, eng="s"):
-            put(eng, ("nc", q, m, part), [("m", G * q + G - 1, NOPE, part)], nope_copy, q, m, part, eng)
+        def I(n, s, eng="v"):
+            put(eng, ("gr", n, s), wid(n, s), interleave, n, s, eng)
+
+        def PI(n):
+            put("t", ("il", n), wid(n, NOPE), pe_interleave, n)
+
+        def E(n, eng="s"):
+            put(eng, ("gr", n, NOPE), [("il", n)], pe_evacuate, n, eng)
+
+        def Q(n, s):
+            put("v", ("q", n, s), [("gr", n, s)], quantize, n, s)
+
+        def MR(n):
+            put("t", ("mr", n), [("q", n, ROPE), ("xq",)], multiply, n, ROPE)
+
+        def MN(n, ms=range(MT)):
+            put("t", ("mn", n), [("q", n, NOPE), ("xq",)], multiply, n, NOPE, ms)
+
+        def NP(q, m):
+            put("t", ("np", q, m), [("q", G * q + g, NOPE) for g in range(G)] + [("xq",)], nope_passes, q, m)
+
+        def NC(q, m, eng="s"):
+            put(eng, ("nc", q, m), [("mn", LAST_NOPE[-1])] if q == QUADS - 1 else [("mn", G * q + G - 1)] if m < 2 else [("np", q, m)], nope_copy, q, m, eng)
 
         def XT(mp):
             put("t", ("xt", mp), [], x_turn, mp)
@@ -269,69 +326,154 @@ def tile_multiheadlatentattention_pb_kernel(tc, x, freq_cis, Wq_bytes, Wq_scale,
             put("v", ("xq",), [("xo", mp, g) for mp in range(2) for g in range(G)], x_quantize)
 
         def RM(q, m):
-            put("v", ("rm", q, m), [("m", G * q + G - 1, ROPE, None), ("tab",)], rope_mul, q, m)
+            put("v", ("rm", q, m), [("mr", G * q + G - 1), ("tab",)], rope_mul, q, m)
 
         def RA(q, m, eng="g"):
             put(eng, ("ra", q, m), [("rm", q, m)], rope_add, q, m, eng)
 
-        def ST(q, m, lo, hi, part=None):
-            put("d", ("st", q, m, lo, part), ([("nc", q, m, part)] if lo == 0 else []) + ([("ra", q, m)] if hi == HD else []),
-                store, q, m, lo, hi, part)
+        def ST(q, m, lo, hi):
+            put("d", ("st", q, m, lo), ([("nc", q, m)] if lo == 0 else []) + ([("ra", q, m)] if hi == HD else []), store, q, m, lo, hi)
 
-        last_parts = range(PARTS) if PARTS > 1 else (None,)
-        for n in range(UNITS):
+        for n in range(LAST):
             W(n)
             q, g = divmod(n, G)
-            if n - S_LAG in S_EARLY:
-                I(n - S_LAG, NOPE, None, "s")
-            if g == G - 1 and q >= 1:
-                for m in range(NV):
-                    NC(q - 1, m)
-        for n in range(LAST, UNITS):
-            I(n, NOPE, None, "s")
-        for n in range(UNITS):
-            if n < 2:
-                WV(n)
-        order = [(n, s) for n in range(LAST) for s in (NOPE, ROPE)] + [(n, ROPE) for n in range(LAST, UNITS)]
-        for j in range(len(order) + 1):
-            if j < len(order) and not (order[j][1] == NOPE and order[j][0] in S_EARLY):
-                I(*order[j])
-            if j % 2 == 0 and 2 + j // 2 < UNITS:
-                WV(2 + j // 2)
-            if j >= 1:
-                Q(*order[j - 1])
-            if j == 2:
-                XO(0)
-            if j == 3:
-                XO(1)
-                XQ()
-            if j >= 2 and order[j - 2][1] == ROPE and order[j - 2][0] % G == G - 1 and j - 2 < len(order) - 1:
-                for m in range(MT):
-                    RM(order[j - 2][0] // G, m)
-                for m in range(NV, MT):
-                    NC(order[j - 2][0] // G, m, None, "v")
-        Q(LAST, NOPE, last_parts[0])
+            if n - 2 in PE_BLOCKS:
+                E(n - 2)
+            if q >= 1 and g >= 2:
+                NC(q - 1, 2 * g - 4)
+                NC(q - 1, 2 * g - 3)
+        E(10)
+        WH(12, ROPE)
+        WH(13, ROPE)
+        E(11)
+        WH(14, ROPE)
+        WH(15, ROPE)
+        NC(2, 0)
+        NC(2, 1)
+        WH(12, NOPE)
+        NC(2, 2)
+        NC(2, 3)
+        WH(13, NOPE)
+        WH(14, NOPE)
+        E(12)
+        WH(15, NOPE)
+        E(13)
+        I(15, NOPE, "s")
+        E(14)
+        WV(0)
+        WV(1)
+        I(0, ROPE)
+        I(0, NOPE)
+        Q(0, ROPE)
+        Q(0, NOPE)
+        WV(2)
+        XO(0)
+        I(1, ROPE)
+        XO(1, (0, 1))
+        Q(1, ROPE)
+        WV(3)
+        XO(1, (2, 3))
+        I(2, ROPE)
+        XQ()
+        Q(1, NOPE)
+        Q(2, ROPE)
+        WV(4)
+        I(3, ROPE)
+        WV(5)
+        Q(2, NOPE)
+        Q(3, ROPE)
+        for q in range(1, QUADS - 1):
+            u = G * q
+            I(u, ROPE)
+            Q(u - 1, NOPE)
+            WV(u + 2)
+            for m in range(MT):
+                RM(q - 1, m)
+            I(u, NOPE)
+            Q(u, ROPE)
+            WV(u + 3)
+            I(u + 1, ROPE)
+            Q(u, NOPE)
+            WV(u + 4)
+            Q(u + 1, ROPE)
+            I(u + 2, ROPE)
+            Q(u + 1, NOPE)
+            Q(u + 2, ROPE)
+            I(u + 3, ROPE)
+            WV(u + 5)
+            Q(u + 2, NOPE)
+            Q(u + 3, ROPE)
+        WVH(12, ROPE)
+        WVH(13, ROPE)
+        I(12, ROPE)
+        Q(11, NOPE)
+        WVH(14, ROPE)
+        Q(12, ROPE)
+        for m in range(MT):
+            RM(2, m)
+        I(13, ROPE)
+        WVH(15, ROPE)
+        I(14, ROPE)
+        Q(13, ROPE)
+        WVH(12, NOPE)
+        I(15, ROPE)
+        Q(14, ROPE)
+        WVH(13, NOPE)
+        Q(15, ROPE)
+        WVH(14, NOPE)
+        WVH(15, NOPE)
+        Q(12, NOPE)
         RM(3, 0)
         RM(3, 1)
-        Q(13, NOPE, last_parts[0])
         RM(3, 2)
-        Q(14, NOPE, last_parts[0])
+        Q(13, NOPE)
         RM(3, 3)
-        Q(15, NOPE, last_parts[0])
+        Q(15, NOPE)
         RA(3, 3, "v")
-        for part in last_parts[1:]:
-            for n in range(LAST, UNITS):
-                Q(n, NOPE, part)
-        for part in last_parts:
-            for m in range(MT):
-                NC(3, m, part, "v" if m % 2 else "s")
+        Q(14, NOPE)
+        NC(3, 1, "v")
+        NC(3, 3, "v")
+        NC(3, 0)
+        NC(3, 2)
         XT(0)
+        PI(1)
         XT(1)
-        for n, s in order:
-            M(n, s)
-        for part in last_parts:
-            for n in range(LAST, UNITS):
-                M(n, NOPE, part)
+        PI(2)
+        MR(0)
+        MN(0, (0, 1))
+        PI(3)
+        MR(1)
+        MN(1, (0, 1))
+        MR(2)
+        MR(3)
+        for q in range(1, QUADS):
+            u = G * q
+            last = q == QUADS - 1
+            MN(u - 2, (0, 1))
+            MN(u - 1, (0, 1))
+            if not last:
+                PI(u + 1)
+            NP(q - 1, 2)
+            NP(q - 1, 3)
+            if not last:
+                PI(u + 2)
+            MR(u)
+            if not last:
+                MN(u, (0, 1))
+                PI(u + 3)
+            else:
+                PI(12)
+            MR(u + 1)
+            if not last:
+                MN(u + 1, (0, 1))
+            MR(u + 2)
+            MR(u + 3)
+        PI(13)
+        MN(12)
+        PI(14)
+        MN(13)
+        MN(15)
+        MN(14)
         put("g", ("tab",), [], tables)
         for q in range(QUADS):
             for m in range(MT):
@@ -342,9 +484,8 @@ def tile_multiheadlatentattention_pb_kernel(tc, x, freq_cis, Wq_bytes, Wq_scale,
                 ST(q, m, 0, HD)
         for m in range(MT):
             ST(3, m, P, HD)
-        for part in last_parts:
-            for m in (0, 1, 2, 3):
-                ST(3, m, 0, P, part)
+        for m in (1, 0, 3, 2):
+            ST(3, m, 0, P)
 
         done = set()
         at = {e: 0 for e in progs}

@@ -25,8 +25,10 @@ UNITS = QUADS * G
 LAST = UNITS - G
 NOPE, ROPE = 0, 1
 PE_BLOCKS = (1, 2, 3, 5, 6, 7, 9, 10, 11, 12, 13, 14)
-VP = tuple(range(2, 12))
-VECTOR_PLANES = ((0, 2), (0, 3), (1, 2), (1, 3)) + tuple((n, 3) for n in VP)
+VECTOR_PLANES = ((0, 2), (0, 3), (1, 2), (1, 3))
+FIRST = ((0, 2, 1, 3), (2, 3, 0, 1))
+CAST = {n: (2, 3) for n in range(2, 12)}
+ELAG = 2
 LAST_NOPE = (12, 13, 15, 14)
 FLOPS = 2 * T * K * HEADS * HD
 
@@ -76,8 +78,8 @@ def tile_multiheadlatentattention_pb_kernel(tc, x, freq_cis, Wq_bytes, Wq_scale,
                 for s in (ROPE, NOPE):
                     for t in range(4):
                         nc.sync.dma_start(out=rows[:, s, t], in_=cols[:, q, s, t])
-            elif n == 0:
-                for t in range(4):
+            elif n < 2:
+                for t in FIRST[n]:
                     nc.sync.dma_start(out=wb[:, t, :], in_=w_view[g, :, t, cols])
             else:
                 nc.sync.dma_start(out=wb[:], in_=w_view[g, :, :, cols])
@@ -111,11 +113,23 @@ def tile_multiheadlatentattention_pb_kernel(tc, x, freq_cis, Wq_bytes, Wq_scale,
                 planes[(n, half)] = pl
             return planes[(n, half)]
 
+        raw = {}
+
         def widen(n, on_vector, half=None):
             q, g = divmod(n, G)
             part = slice(0, 1024) if half is None else slice(512 * half, 512 * (half + 1))
+            width = part.stop - part.start
+            cast = CAST.get(n, ())
+            if cast and not on_vector:
+                rt = pl_pool.tile([P, len(cast), width], BF16, name="raw", tag="raw", bufs=2, align_bytes=64)
+                raw[(n, half)] = rt
+                nc.scalar.copy(out=rt[:], in_=wbytes[n][:, cast[0]:cast[-1] + 1, part].bitcast(FP8))
             for t in range(4):
-                if ((n, t) in VECTOR_PLANES) == on_vector:
+                if t in cast and on_vector:
+                    pl = plane_tile(n, half)
+                    nc.vector.tensor_scalar(out=pl[:, t, :], in0=raw[(n, half)][:, t - cast[0], :], scalar1=wsc[:, g, t:t + 1],
+                                            scalar2=None, op0=MULT)
+                elif t not in cast and ((n, t) in VECTOR_PLANES) == on_vector:
                     pl = plane_tile(n, half)
                     src = wbytes[n][:, t, part].bitcast(FP8)
                     if on_vector:
@@ -272,24 +286,27 @@ def tile_multiheadlatentattention_pb_kernel(tc, x, freq_cis, Wq_bytes, Wq_scale,
         def put(eng, gives, needs, fn, *args):
             progs[eng].append((gives, needs, fn, args))
 
+        def on_v(n):
+            return n in CAST or any(v[0] == n for v in VECTOR_PLANES)
+
         def W(n):
             put("s", ("ws", n), [], widen, n, False)
 
         def WV(n):
-            if n < LAST and any(v[0] == n for v in VECTOR_PLANES):
-                put("v", ("wv", n), [], widen, n, True)
+            if n < LAST and on_v(n):
+                put("v", ("wv", n), [("ws", n)] if n in CAST else [], widen, n, True)
 
         def WH(n, s):
             put("s", ("ws", n, s), [], widen, n, False, s)
 
         def WVH(n, s):
-            if any(v[0] == n for v in VECTOR_PLANES):
-                put("v", ("wv", n, s), [], widen, n, True, s)
+            if on_v(n):
+                put("v", ("wv", n, s), [("ws", n, s)] if n in CAST else [], widen, n, True, s)
 
         def wid(n, s):
             if n >= LAST:
-                return [("ws", n, s)] + ([("wv", n, s)] if any(v[0] == n for v in VECTOR_PLANES) else [])
-            return [("ws", n)] + ([("wv", n)] if any(v[0] == n for v in VECTOR_PLANES) else [])
+                return [("ws", n, s)] + ([("wv", n, s)] if on_v(n) else [])
+            return [("ws", n)] + ([("wv", n)] if on_v(n) else [])
 
         def I(n, s, eng="v"):
             put(eng, ("gr", n, s), wid(n, s), interleave, n, s, eng)
@@ -337,12 +354,13 @@ def tile_multiheadlatentattention_pb_kernel(tc, x, freq_cis, Wq_bytes, Wq_scale,
         for n in range(LAST):
             W(n)
             q, g = divmod(n, G)
-            if n - 2 in PE_BLOCKS:
-                E(n - 2)
+            if n - ELAG in PE_BLOCKS:
+                E(n - ELAG)
             if q >= 1 and g >= 2:
                 NC(q - 1, 2 * g - 4)
                 NC(q - 1, 2 * g - 3)
-        E(10)
+        for n in range(LAST - ELAG, LAST - 1):
+            E(n)
         WH(12, ROPE)
         WH(13, ROPE)
         E(11)
@@ -366,41 +384,39 @@ def tile_multiheadlatentattention_pb_kernel(tc, x, freq_cis, Wq_bytes, Wq_scale,
         I(0, NOPE)
         Q(0, ROPE)
         Q(0, NOPE)
-        WV(2)
-        XO(0)
         I(1, ROPE)
-        XO(1, (0, 1))
+        XO(0)
+        WV(2)
         Q(1, ROPE)
-        WV(3)
-        XO(1, (2, 3))
         I(2, ROPE)
+        WV(3)
+        XO(1)
         XQ()
         Q(1, NOPE)
         Q(2, ROPE)
-        WV(4)
         I(3, ROPE)
-        WV(5)
+        WV(4)
         Q(2, NOPE)
         Q(3, ROPE)
         for q in range(1, QUADS - 1):
             u = G * q
             I(u, ROPE)
+            WV(u + 1)
             Q(u - 1, NOPE)
-            WV(u + 2)
             for m in range(MT):
                 RM(q - 1, m)
+            WV(u + 2)
             I(u, NOPE)
             Q(u, ROPE)
-            WV(u + 3)
             I(u + 1, ROPE)
             Q(u, NOPE)
-            WV(u + 4)
             Q(u + 1, ROPE)
             I(u + 2, ROPE)
+            WV(u + 3)
             Q(u + 1, NOPE)
             Q(u + 2, ROPE)
             I(u + 3, ROPE)
-            WV(u + 5)
+            WV(u + 4)
             Q(u + 2, NOPE)
             Q(u + 3, ROPE)
         WVH(12, ROPE)
@@ -422,12 +438,12 @@ def tile_multiheadlatentattention_pb_kernel(tc, x, freq_cis, Wq_bytes, Wq_scale,
         Q(15, ROPE)
         WVH(14, NOPE)
         WVH(15, NOPE)
-        Q(12, NOPE)
         RM(3, 0)
         RM(3, 1)
+        Q(12, NOPE)
         RM(3, 2)
-        Q(13, NOPE)
         RM(3, 3)
+        Q(13, NOPE)
         Q(15, NOPE)
         RA(3, 3, "v")
         Q(14, NOPE)
@@ -435,8 +451,8 @@ def tile_multiheadlatentattention_pb_kernel(tc, x, freq_cis, Wq_bytes, Wq_scale,
         NC(3, 3, "v")
         NC(3, 0)
         NC(3, 2)
-        XT(0)
         PI(1)
+        XT(0)
         XT(1)
         PI(2)
         MR(0)

@@ -27,7 +27,7 @@ NOPE, ROPE = 0, 1
 PE_BLOCKS = (1, 2, 3, 5, 6, 7, 9, 10, 11, 12, 13, 14)
 VECTOR_PLANES = ((0, 2), (0, 3), (1, 2), (1, 3))
 FIRST = ((0, 2, 1, 3), (2, 3, 0, 1))
-CAST = {n: (2, 3) for n in range(2, 12)}
+CAST = {**{(n, None): (2,3) for n in (2,3,4,5,6,7,8)}, **{(n, None): (1,2,3) for n in (9,10,11)}, **{k: (0,1,2,3) for k in ((14,0),)}}
 ELAG = 2
 LAST_NOPE = (12, 13, 15, 14)
 FLOPS = 2 * T * K * HEADS * HD
@@ -42,7 +42,7 @@ def tile_multiheadlatentattention_pb_kernel(tc, x, freq_cis, Wq_bytes, Wq_scale,
     with ExitStack() as ctx:
         ctx.enter_context(tc.manual_schedule())
         const = ctx.enter_context(tc.tile_pool(name="const", bufs=1))
-        wb_pool = ctx.enter_context(tc.tile_pool(name="wbytes", bufs=11))
+        wb_pool = ctx.enter_context(tc.tile_pool(name="wbytes", bufs=10))
         pl_pool = ctx.enter_context(tc.tile_pool(name="planes", bufs=7))
         gr_pool = ctx.enter_context(tc.tile_pool(name="grouped", bufs=4))
         wc_pool = ctx.enter_context(tc.tile_pool(name="wcodes", bufs=9))
@@ -70,15 +70,17 @@ def tile_multiheadlatentattention_pb_kernel(tc, x, freq_cis, Wq_bytes, Wq_scale,
         def load_w(n):
             q, g = divmod(n, G)
             cols = slice(1024 * q, 1024 * (q + 1))
-            wb = wb_pool.tile([P, 4, 1024], U8, name="wb", tag="wb")
-            wbytes[n] = wb
             if n >= LAST:
-                rows = wb[:].rearrange("p t (s h f) -> p s t h f", s=2, h=4)
-                cols = w_view[g].rearrange("p t (q h s f) -> p q s t h f", q=QUADS, h=4, s=2)
+                by_half = w_view[g].rearrange("p t (q h s f) -> p q s t h f", q=QUADS, h=4, s=2)
                 for s in (ROPE, NOPE):
+                    wb = wb_pool.tile([P, 4, 512], U8, name="wb", tag="wb")
+                    wbytes[(n, s)] = wb
                     for t in range(4):
-                        nc.sync.dma_start(out=rows[:, s, t], in_=cols[:, q, s, t])
-            elif n < 2:
+                        nc.sync.dma_start(out=wb[:, t].rearrange("p (h f) -> p h f", h=4), in_=by_half[:, q, s, t])
+                return
+            wb = wb_pool.tile([P, 4, 1024], U8, name="wb", tag="wb")
+            wbytes[(n, None)] = wb
+            if n < 2:
                 for t in FIRST[n]:
                     nc.sync.dma_start(out=wb[:, t, :], in_=w_view[g, :, t, cols])
             else:
@@ -117,13 +119,12 @@ def tile_multiheadlatentattention_pb_kernel(tc, x, freq_cis, Wq_bytes, Wq_scale,
 
         def widen(n, on_vector, half=None):
             q, g = divmod(n, G)
-            part = slice(0, 1024) if half is None else slice(512 * half, 512 * (half + 1))
-            width = part.stop - part.start
-            cast = CAST.get(n, ())
+            width = 1024 if half is None else 512
+            cast = CAST.get((n, half), ())
             if cast and not on_vector:
                 rt = pl_pool.tile([P, len(cast), width], BF16, name="raw", tag="raw", bufs=2, align_bytes=64)
                 raw[(n, half)] = rt
-                nc.scalar.copy(out=rt[:], in_=wbytes[n][:, cast[0]:cast[-1] + 1, part].bitcast(FP8))
+                nc.scalar.copy(out=rt[:], in_=wbytes[(n, half)][:, cast[0]:cast[-1] + 1, :].bitcast(FP8))
             for t in range(4):
                 if t in cast and on_vector:
                     pl = plane_tile(n, half)
@@ -131,7 +132,7 @@ def tile_multiheadlatentattention_pb_kernel(tc, x, freq_cis, Wq_bytes, Wq_scale,
                                             scalar2=None, op0=MULT)
                 elif t not in cast and ((n, t) in VECTOR_PLANES) == on_vector:
                     pl = plane_tile(n, half)
-                    src = wbytes[n][:, t, part].bitcast(FP8)
+                    src = wbytes[(n, half)][:, t, :].bitcast(FP8)
                     if on_vector:
                         nc.vector.tensor_scalar(out=pl[:, t, :], in0=src, scalar1=wsc[:, g, t:t + 1],
                                                 scalar2=None, op0=MULT)
@@ -181,27 +182,37 @@ def tile_multiheadlatentattention_pb_kernel(tc, x, freq_cis, Wq_bytes, Wq_scale,
 
         codes = {}
 
+        def cols_of(s):
+            return {"a": slice(0, 256), "b": slice(256, 512)}.get(s, slice(0, 512))
+
         def quantize(n, s):
+            kept = ROPE if s == ROPE else NOPE
             depth = 5 if s == ROPE else 7
-            wc = wc_pool.tile([P, 512], U32, name="wc", tag="wc%d" % s, bufs=depth, align_bytes=64)
-            ws = wc_pool.tile([P, 512], U8, name="ws", tag="ws%d" % s, bufs=depth, align_bytes=64)
-            codes[(n, s)] = (wc, ws)
-            nc.vector.quantize_mx(out=wc[:].bitcast(FP8X4), scales=ws[:], in_=grouped[(n, s)][:])
+            if (n, kept) not in codes:
+                wc = wc_pool.tile([P, 512], U32, name="wc", tag="wc%d" % kept, bufs=depth, align_bytes=64)
+                ws = wc_pool.tile([P, 512], U8, name="ws", tag="ws%d" % kept, bufs=depth, align_bytes=64)
+                codes[(n, kept)] = (wc, ws)
+            wc, ws = codes[(n, kept)]
+            cols = cols_of(s)
+            nc.vector.quantize_mx(out=wc[:, cols].bitcast(FP8X4), scales=ws[:, cols],
+                                  in_=grouped[(n, kept)][:, 4 * cols.start:4 * cols.stop])
 
         acc = {}
 
         def one_pass(n, s, m):
             q, g = divmod(n, G)
-            rank = LAST_NOPE.index(n) if n >= LAST and s == NOPE else g
-            wc, ws = codes[(n, s)]
+            kept = ROPE if s == ROPE else NOPE
+            rank = LAST_NOPE.index(n) if n >= LAST and kept == NOPE else g
+            wc, ws = codes[(n, kept)]
+            cols = cols_of(s)
             if rank == 0:
-                tag = "rope" if s == ROPE or (q == QUADS - 1 and m >= 2) else "nope"
+                tag = {ROPE: "rope", NOPE: "nope", "a": "nope" if m < 2 else "rope", "b": "rope" if m < 2 else "il"}[s]
                 bank = psum.tile([P, 512], F32, name="bank", tag=tag, bufs=4 if tag == "rope" else 2)
                 acc[(q, s, m)] = bank
             toks = slice(P * m, P * (m + 1))
-            nc.tensor.matmul_mx(out=acc[(q, s, m)][:],
+            nc.tensor.matmul_mx(out=acc[(q, s, m)][:, cols],
                                 lhsT=xc[:, g, toks].bitcast(FP8X4), lhsT_scale=xs[:, g, toks],
-                                rhs=wc[:].bitcast(FP8X4), rhs_scale=ws[:],
+                                rhs=wc[:, cols].bitcast(FP8X4), rhs_scale=ws[:, cols],
                                 start=(rank == 0), stop=(rank == G - 1))
 
         def multiply(n, s, ms=range(MT)):
@@ -270,42 +281,48 @@ def tile_multiheadlatentattention_pb_kernel(tc, x, freq_cis, Wq_bytes, Wq_scale,
                 in0=t1[:].rearrange("p (h i e) -> p h i e", h=4, e=2),
                 in1=t2[:].rearrange("p (h i e) -> p h i e", h=4, e=2)[:, :, :, ::-1], op=ADD)
 
-        def store(q, m, lo, hi):
-            nc.sync.dma_start(out=out_view[m][:, 4 * q:4 * (q + 1), lo:hi], in_=staged[(q, m)][:, :, lo:hi])
+        def heads_of(s):
+            return {"a": slice(0, 2), "b": slice(2, 4)}.get(s, slice(0, 4))
 
-        def nope_copy(q, m, eng="s"):
+        def store(q, m, lo, hi, s):
+            hs = heads_of(s)
+            nc.sync.dma_start(out=out_view[m][:, 4 * q + hs.start:4 * q + hs.stop, lo:hi],
+                              in_=staged[(q, m)][:, hs, lo:hi])
+
+        def nope_copy(q, m, eng, s):
             ost = stage_tile(q, m)
-            src = acc[(q, NOPE, m)][:].rearrange("p (h f) -> p h f", h=4)
+            hs = heads_of(s)
+            src = acc[(q, s, m)][:].rearrange("p (h f) -> p h f", h=4)[:, hs]
             if eng == "v":
-                nc.vector.tensor_copy(out=ost[:, :, 0:P], in_=src)
+                nc.vector.tensor_copy(out=ost[:, hs, 0:P], in_=src)
             else:
-                nc.scalar.copy(out=ost[:, :, 0:P], in_=src)
+                nc.scalar.copy(out=ost[:, hs, 0:P], in_=src)
 
         progs = {"s": [], "t": [], "v": [], "g": [], "d": []}
 
         def put(eng, gives, needs, fn, *args):
             progs[eng].append((gives, needs, fn, args))
 
-        def on_v(n):
-            return n in CAST or any(v[0] == n for v in VECTOR_PLANES)
+        def on_v(n, s=None):
+            return (n, s) in CAST or any(v[0] == n for v in VECTOR_PLANES)
 
         def W(n):
             put("s", ("ws", n), [], widen, n, False)
 
         def WV(n):
             if n < LAST and on_v(n):
-                put("v", ("wv", n), [("ws", n)] if n in CAST else [], widen, n, True)
+                put("v", ("wv", n), [("ws", n)] if (n, None) in CAST else [], widen, n, True)
 
         def WH(n, s):
             put("s", ("ws", n, s), [], widen, n, False, s)
 
         def WVH(n, s):
-            if on_v(n):
-                put("v", ("wv", n, s), [("ws", n, s)] if n in CAST else [], widen, n, True, s)
+            if on_v(n, s):
+                put("v", ("wv", n, s), [("ws", n, s)], widen, n, True, s)
 
         def wid(n, s):
             if n >= LAST:
-                return [("ws", n, s)] + ([("wv", n, s)] if on_v(n) else [])
+                return [("ws", n, s)] + ([("wv", n, s)] if on_v(n, s) else [])
             return [("ws", n)] + ([("wv", n)] if on_v(n) else [])
 
         def I(n, s, eng="v"):
@@ -318,19 +335,25 @@ def tile_multiheadlatentattention_pb_kernel(tc, x, freq_cis, Wq_bytes, Wq_scale,
             put(eng, ("gr", n, NOPE), [("il", n)], pe_evacuate, n, eng)
 
         def Q(n, s):
-            put("v", ("q", n, s), [("gr", n, s)], quantize, n, s)
+            put("v", ("q", n, s), [("gr", n, ROPE if s == ROPE else NOPE)], quantize, n, s)
 
         def MR(n):
             put("t", ("mr", n), [("q", n, ROPE), ("xq",)], multiply, n, ROPE)
 
-        def MN(n, ms=range(MT)):
-            put("t", ("mn", n), [("q", n, NOPE), ("xq",)], multiply, n, NOPE, ms)
+        def MN(n, ms=range(MT), s=NOPE):
+            put("t", ("mn", n, s), [("q", n, s), ("xq",)], multiply, n, s, ms)
 
         def NP(q, m):
             put("t", ("np", q, m), [("q", G * q + g, NOPE) for g in range(G)] + [("xq",)], nope_passes, q, m)
 
-        def NC(q, m, eng="s"):
-            put(eng, ("nc", q, m), [("mn", LAST_NOPE[-1])] if q == QUADS - 1 else [("mn", G * q + G - 1)] if m < 2 else [("np", q, m)], nope_copy, q, m, eng)
+        def NC(q, m, eng="s", s=NOPE):
+            if q == QUADS - 1:
+                needs = [("mn", LAST_NOPE[-1], s)]
+            elif m < 2:
+                needs = [("mn", G * q + G - 1, NOPE)]
+            else:
+                needs = [("np", q, m)]
+            put(eng, ("nc", q, m, s), needs, nope_copy, q, m, eng, s)
 
         def XT(mp):
             put("t", ("xt", mp), [], x_turn, mp)
@@ -348,8 +371,8 @@ def tile_multiheadlatentattention_pb_kernel(tc, x, freq_cis, Wq_bytes, Wq_scale,
         def RA(q, m, eng="g"):
             put(eng, ("ra", q, m), [("rm", q, m)], rope_add, q, m, eng)
 
-        def ST(q, m, lo, hi):
-            put("d", ("st", q, m, lo), ([("nc", q, m)] if lo == 0 else []) + ([("ra", q, m)] if hi == HD else []), store, q, m, lo, hi)
+        def ST(q, m, lo, hi, s=NOPE):
+            put("d", ("st", q, m, lo, s), ([("nc", q, m, s)] if lo == 0 else []) + ([("ra", q, m)] if hi == HD else []), store, q, m, lo, hi, s)
 
         for n in range(LAST):
             W(n)
@@ -385,8 +408,8 @@ def tile_multiheadlatentattention_pb_kernel(tc, x, freq_cis, Wq_bytes, Wq_scale,
         Q(0, ROPE)
         Q(0, NOPE)
         I(1, ROPE)
-        XO(0)
         WV(2)
+        XO(0)
         Q(1, ROPE)
         I(2, ROPE)
         WV(3)
@@ -431,26 +454,29 @@ def tile_multiheadlatentattention_pb_kernel(tc, x, freq_cis, Wq_bytes, Wq_scale,
         WVH(15, ROPE)
         I(14, ROPE)
         Q(13, ROPE)
-        WVH(12, NOPE)
         I(15, ROPE)
         Q(14, ROPE)
-        WVH(13, NOPE)
         Q(15, ROPE)
         WVH(14, NOPE)
-        WVH(15, NOPE)
         RM(3, 0)
+        Q(12, "a")
+        Q(12, "b")
         RM(3, 1)
-        Q(12, NOPE)
         RM(3, 2)
+        Q(13, "a")
+        Q(13, "b")
         RM(3, 3)
-        Q(13, NOPE)
-        Q(15, NOPE)
+        Q(15, "a")
         RA(3, 3, "v")
-        Q(14, NOPE)
-        NC(3, 1, "v")
-        NC(3, 3, "v")
-        NC(3, 0)
-        NC(3, 2)
+        Q(14, "a")
+        Q(15, "b")
+        Q(14, "b")
+        NC(3, 1, "v", "a")
+        NC(3, 3, "v", "a")
+        NC(3, 0, "s", "a")
+        NC(3, 2, "s", "a")
+        for m in range(MT):
+            NC(3, m, "v" if m % 2 else "s", "b")
         PI(1)
         XT(0)
         XT(1)
@@ -485,11 +511,13 @@ def tile_multiheadlatentattention_pb_kernel(tc, x, freq_cis, Wq_bytes, Wq_scale,
             MR(u + 2)
             MR(u + 3)
         PI(13)
-        MN(12)
+        MN(12, range(MT), "a")
         PI(14)
-        MN(13)
-        MN(15)
-        MN(14)
+        MN(13, range(MT), "a")
+        MN(15, range(MT), "a")
+        MN(14, range(MT), "a")
+        for n in LAST_NOPE:
+            MN(n, range(MT), "b")
         put("g", ("tab",), [], tables)
         for q in range(QUADS):
             for m in range(MT):
@@ -500,8 +528,9 @@ def tile_multiheadlatentattention_pb_kernel(tc, x, freq_cis, Wq_bytes, Wq_scale,
                 ST(q, m, 0, HD)
         for m in range(MT):
             ST(3, m, P, HD)
-        for m in (1, 0, 3, 2):
-            ST(3, m, 0, P)
+        for s in ("a", "b"):
+            for m in range(MT):
+                ST(3, m, 0, P, s)
 
         done = set()
         at = {e: 0 for e in progs}

from contextlib import ExitStack

import concourse.mybir as mybir
from concourse.masks import make_identity

F32 = mybir.dt.float32
BF16 = mybir.dt.bfloat16
U32 = mybir.dt.uint32
U8 = mybir.dt.uint8
FP8 = mybir.dt.float8_e4m3fn
FP8X4 = mybir.dt.float8_e4m3fn_x4
MULT = mybir.AluOpType.mult
ADD = mybir.AluOpType.add
COPY = mybir.ActivationFunctionType.Copy

P = 128
T = 512
K = 2048
HEADS = 16
HD = 256
G = K // 512
MT = T // P
QUADS = 4
UNITS = QUADS * G
LAST = UNITS - G
NOPE, ROPE = 0, 1
PE_BLOCKS = (1, 2, 3, 5, 6, 7, 9, 10, 11, 12, 13, 14)
VECTOR_PLANES = ((0, 2), (0, 3), (1, 2), (1, 3))
FIRST = ((0, 2, 1, 3), (2, 3, 0, 1))
CAST = {**{(n, None): (2,3) for n in (2,3,4,5,6,7,8)}, **{(n, None): (1,2,3) for n in (9,10,11)}, **{k: (0,1,2,3) for k in ((14,0),)}}
ELAG = 2
LAST_NOPE = (12, 13, 15, 14)
FLOPS = 2 * T * K * HEADS * HD


def tile_multiheadlatentattention_pb_kernel(tc, x, freq_cis, Wq_bytes, Wq_scale, out):
    nc = tc.nc
    w_view = Wq_bytes.rearrange("(g p t) n -> g p t n", p=P, t=4)
    x_view = x.rearrange("b (m p) k -> (b m) p k", p=P)
    out_view = out.rearrange("b (m p) h d -> (b m) p h d", p=P)

    with ExitStack() as ctx:
        ctx.enter_context(tc.manual_schedule())
        const = ctx.enter_context(tc.tile_pool(name="const", bufs=1))
        wb_pool = ctx.enter_context(tc.tile_pool(name="wbytes", bufs=10))
        pl_pool = ctx.enter_context(tc.tile_pool(name="planes", bufs=7))
        gr_pool = ctx.enter_context(tc.tile_pool(name="grouped", bufs=4))
        wc_pool = ctx.enter_context(tc.tile_pool(name="wcodes", bufs=9))
        ost_pool = ctx.enter_context(tc.tile_pool(name="ost", bufs=8))
        tmp_pool = ctx.enter_context(tc.tile_pool(name="tmp", bufs=4))
        psum = ctx.enter_context(tc.psum_pool(name="psum", bufs=4))

        wsc = const.tile([P, G, 4], F32, name="wsc")
        nc.scalar.dma_start(out=wsc[:], in_=Wq_scale.rearrange("(g p t) o -> p g (t o)", p=P, t=4))
        warm = const.tile([P, 2], F32, name="warm")
        nc.vector.memset(warm[:], 0.0)
        nc.scalar.activation(out=warm[:, 1:2], in_=warm[:, 0:1], func=COPY)
        ident = const.tile([P, P], F32, name="ident")
        make_identity(nc, ident[:])
        ident_bf = const.tile([P, P], BF16, name="ident_bf")
        make_identity(nc, ident_bf[:])
        fc = const.tile([P, MT, P], BF16, name="fc")
        cos2 = const.tile([P, MT, P], F32, name="cos2")
        sin2 = const.tile([P, MT, P], F32, name="sin2")
        xc = const.tile([P, G, T], U32, name="xc", align_bytes=64)
        xs = const.tile([P, G, T], U8, name="xs", align_bytes=64)

        wbytes = {}

        def load_w(n):
            q, g = divmod(n, G)
            cols = slice(1024 * q, 1024 * (q + 1))
            if n >= LAST:
                by_half = w_view[g].rearrange("p t (q h s f) -> p q s t h f", q=QUADS, h=4, s=2)
                for s in (ROPE, NOPE):
                    wb = wb_pool.tile([P, 4, 512], U8, name="wb", tag="wb")
                    wbytes[(n, s)] = wb
                    for t in range(4):
                        nc.sync.dma_start(out=wb[:, t].rearrange("p (h f) -> p h f", h=4), in_=by_half[:, q, s, t])
                return
            wb = wb_pool.tile([P, 4, 1024], U8, name="wb", tag="wb")
            wbytes[(n, None)] = wb
            if n < 2:
                for t in FIRST[n]:
                    nc.sync.dma_start(out=wb[:, t, :], in_=w_view[g, :, t, cols])
            else:
                nc.sync.dma_start(out=wb[:], in_=w_view[g, :, :, cols])

        x_tiles = {}

        def load_x(m):
            x_sb = ost_pool.tile([P, K], BF16, name="x_sb", tag="ost", align_bytes=64)
            x_tiles[m] = x_sb
            nc.sync.dma_start(out=x_sb[:], in_=x_view[m])

        for what, idx in (("w", 0), ("w", 1), ("w", 2), ("x", 0), ("x", 1), ("x", 2), ("w", 3), ("x", 3), ("f", 0)):
            if what == "w":
                load_w(idx)
            elif what == "f":
                nc.sync.dma_start(out=fc[:], in_=freq_cis.rearrange("(m p) i c -> p m (i c)", p=P))
            else:
                load_x(idx)
        for n in range(4, UNITS):
            load_w(n)
        xg = {}
        for g in range(G):
            xgt = ost_pool.tile([P, T, 2], F32, name="xg", tag="ost", align_bytes=64)
            xg[g] = xgt

        planes = {}

        def plane_tile(n, half):
            if (n, half) not in planes:
                pl = pl_pool.tile([P, 4, 1024 if half is None else 512], BF16, name="pl", tag="pl", align_bytes=64)
                planes[(n, half)] = pl
            return planes[(n, half)]

        raw = {}

        def widen(n, on_vector, half=None):
            q, g = divmod(n, G)
            width = 1024 if half is None else 512
            cast = CAST.get((n, half), ())
            if cast and not on_vector:
                rt = pl_pool.tile([P, len(cast), width], BF16, name="raw", tag="raw", bufs=2, align_bytes=64)
                raw[(n, half)] = rt
                nc.scalar.copy(out=rt[:], in_=wbytes[(n, half)][:, cast[0]:cast[-1] + 1, :].bitcast(FP8))
            for t in range(4):
                if t in cast and on_vector:
                    pl = plane_tile(n, half)
                    nc.vector.tensor_scalar(out=pl[:, t, :], in0=raw[(n, half)][:, t - cast[0], :], scalar1=wsc[:, g, t:t + 1],
                                            scalar2=None, op0=MULT)
                elif t not in cast and ((n, t) in VECTOR_PLANES) == on_vector:
                    pl = plane_tile(n, half)
                    src = wbytes[(n, half)][:, t, :].bitcast(FP8)
                    if on_vector:
                        nc.vector.tensor_scalar(out=pl[:, t, :], in0=src, scalar1=wsc[:, g, t:t + 1],
                                                scalar2=None, op0=MULT)
                    else:
                        nc.scalar.activation(out=pl[:, t, :], in_=src, func=COPY, scale=wsc[:, g, t:t + 1])

        grouped = {}

        def group_tile(n, s, made_by):
            gr = gr_pool.tile([P, 2048], BF16, name="gr", tag="gr" + made_by, bufs=4, align_bytes=64)
            grouped[(n, s)] = gr
            return gr

        def half_of(n, s):
            if n < LAST:
                return planes[(n, None)][:].rearrange("p t (h s a i) -> p s h a t i", s=2, a=16, i=8)[:, s]
            return planes[(n, s)][:].rearrange("p t (h a i) -> p h a t i", a=16, i=8)

        def interleave(n, s, eng="v"):
            gr = group_tile(n, s, "v" if eng == "v" else "s")
            dst = gr[:].rearrange("p (h a i t) -> p h a t i", h=4, i=8, t=4)
            src = half_of(n, s)
            if eng == "v":
                nc.vector.tensor_copy(out=dst, in_=src)
            else:
                nc.scalar.copy(out=dst, in_=src)

        woven = {}

        def pe_interleave(n):
            src = half_of(n, NOPE)
            for b in range(2):
                il = psum.tile([P, 1024], BF16, name="il", tag="il", bufs=2)
                woven[(n, b)] = il
                for hh in range(2):
                    nc.tensor.matmul(out=il[:, 512 * hh:512 * (hh + 1)].rearrange("p (a i t) -> p a t i", i=8, t=4),
                                     lhsT=ident_bf[:], rhs=src[:, 2 * b + hh], start=True, stop=True)

        def pe_evacuate(n, eng="s"):
            gr = group_tile(n, NOPE, eng)
            for b in range(2):
                dst = gr[:, 1024 * b:1024 * (b + 1)]
                if eng == "v":
                    nc.vector.tensor_copy(out=dst, in_=woven[(n, b)][:])
                else:
                    nc.scalar.copy(out=dst, in_=woven[(n, b)][:])

        codes = {}

        def cols_of(s):
            return {"a": slice(0, 256), "b": slice(256, 512)}.get(s, slice(0, 512))

        def quantize(n, s):
            kept = ROPE if s == ROPE else NOPE
            depth = 5 if s == ROPE else 7
            if (n, kept) not in codes:
                wc = wc_pool.tile([P, 512], U32, name="wc", tag="wc%d" % kept, bufs=depth, align_bytes=64)
                ws = wc_pool.tile([P, 512], U8, name="ws", tag="ws%d" % kept, bufs=depth, align_bytes=64)
                codes[(n, kept)] = (wc, ws)
            wc, ws = codes[(n, kept)]
            cols = cols_of(s)
            nc.vector.quantize_mx(out=wc[:, cols].bitcast(FP8X4), scales=ws[:, cols],
                                  in_=grouped[(n, kept)][:, 4 * cols.start:4 * cols.stop])

        acc = {}

        def one_pass(n, s, m):
            q, g = divmod(n, G)
            kept = ROPE if s == ROPE else NOPE
            rank = LAST_NOPE.index(n) if n >= LAST and kept == NOPE else g
            wc, ws = codes[(n, kept)]
            cols = cols_of(s)
            if rank == 0:
                tag = {ROPE: "rope", NOPE: "nope", "a": "nope" if m < 2 else "rope", "b": "rope" if m < 2 else "il"}[s]
                bank = psum.tile([P, 512], F32, name="bank", tag=tag, bufs=4 if tag == "rope" else 2)
                acc[(q, s, m)] = bank
            toks = slice(P * m, P * (m + 1))
            nc.tensor.matmul_mx(out=acc[(q, s, m)][:, cols],
                                lhsT=xc[:, g, toks].bitcast(FP8X4), lhsT_scale=xs[:, g, toks],
                                rhs=wc[:, cols].bitcast(FP8X4), rhs_scale=ws[:, cols],
                                start=(rank == 0), stop=(rank == G - 1))

        def multiply(n, s, ms=range(MT)):
            for m in ms:
                one_pass(n, s, m)

        def nope_passes(q, m):
            for g in range(G):
                one_pass(G * q + g, NOPE, m)

        turned = {}

        def x_turn(mp):
            for g in range(G):
                xt = psum.tile([P, 2, 2, P], F32, name="xt", tag="rope", bufs=4)
                turned[(mp, g)] = xt
                for mm in range(2):
                    words = x_tiles[2 * mp + mm][:].bitcast(F32)
                    for u in range(2):
                        nc.tensor.transpose(out=xt[:, mm, u, :], in_=words[:, 256 * g + u:256 * (g + 1):2],
                                            identity=ident[:])

        def x_out(mp, g):
            nc.vector.tensor_copy(out=xg[g][:, 2 * P * mp:2 * P * (mp + 1), :].rearrange("p (m r) u -> p m r u", m=2),
                                  in_=turned[(mp, g)][:].rearrange("p m u r -> p m r u"))

        def x_quantize():
            for g in range(G):
                nc.vector.quantize_mx(out=xc[:, g, :].bitcast(FP8X4), scales=xs[:, g, :],
                                      in_=xg[g][:].rearrange("p r u -> p (r u)").bitcast(BF16))

        def tables():
            fcv = fc[:].rearrange("p m (i c) -> p m i c", c=2)
            c2v = cos2[:].rearrange("p m (i c) -> p m i c", c=2)
            s2v = sin2[:].rearrange("p m (i c) -> p m i c", c=2)
            for dst, c, sign in ((c2v[:, :, :, 0:1], 0, 1.0), (c2v[:, :, :, 1:2], 0, 1.0),
                                 (s2v[:, :, :, 0:1], 1, 1.0), (s2v[:, :, :, 1:2], 1, -1.0)):
                nc.gpsimd.tensor_scalar(out=dst, in0=fcv[:, :, :, c:c + 1], scalar1=sign, scalar2=0.0,
                                        op0=MULT, op1=ADD)

        staged = {}

        def stage_tile(q, m):
            if (q, m) not in staged:
                ost = ost_pool.tile([P, 4, HD], F32, name="ost", tag="ost", align_bytes=64)
                staged[(q, m)] = ost
            return staged[(q, m)]

        prods = {}

        def rope_mul(q, m):
            bank = acc[(q, ROPE, m)]
            t1 = tmp_pool.tile([P, 512], F32, name="t1", tag="t1")
            t2 = tmp_pool.tile([P, 512], F32, name="t2", tag="t2")
            for dst, table in ((t1, cos2), (t2, sin2)):
                nc.vector.tensor_tensor(out=dst[:].rearrange("p (h j) -> p h j", h=4),
                                        in0=bank[:].rearrange("p (h j) -> p h j", h=4),
                                        in1=table[:, m:m + 1, :].to_broadcast([P, 4, P]), op=MULT)
            prods[(q, m)] = (t1, t2)

        def rope_add(q, m, eng="g"):
            t1, t2 = prods[(q, m)]
            ost = stage_tile(q, m)
            (nc.vector if eng == "v" else nc.gpsimd).tensor_tensor(
                out=ost[:, :, P:HD].rearrange("p h (i e) -> p h i e", e=2),
                in0=t1[:].rearrange("p (h i e) -> p h i e", h=4, e=2),
                in1=t2[:].rearrange("p (h i e) -> p h i e", h=4, e=2)[:, :, :, ::-1], op=ADD)

        def heads_of(s):
            return {"a": slice(0, 2), "b": slice(2, 4)}.get(s, slice(0, 4))

        def store(q, m, lo, hi, s):
            hs = heads_of(s)
            nc.sync.dma_start(out=out_view[m][:, 4 * q + hs.start:4 * q + hs.stop, lo:hi],
                              in_=staged[(q, m)][:, hs, lo:hi])

        def nope_copy(q, m, eng, s):
            ost = stage_tile(q, m)
            hs = heads_of(s)
            src = acc[(q, s, m)][:].rearrange("p (h f) -> p h f", h=4)[:, hs]
            if eng == "v":
                nc.vector.tensor_copy(out=ost[:, hs, 0:P], in_=src)
            else:
                nc.scalar.copy(out=ost[:, hs, 0:P], in_=src)

        progs = {"s": [], "t": [], "v": [], "g": [], "d": []}

        def put(eng, gives, needs, fn, *args):
            progs[eng].append((gives, needs, fn, args))

        def on_v(n, s=None):
            return (n, s) in CAST or any(v[0] == n for v in VECTOR_PLANES)

        def W(n):
            put("s", ("ws", n), [], widen, n, False)

        def WV(n):
            if n < LAST and on_v(n):
                put("v", ("wv", n), [("ws", n)] if (n, None) in CAST else [], widen, n, True)

        def WH(n, s):
            put("s", ("ws", n, s), [], widen, n, False, s)

        def WVH(n, s):
            if on_v(n, s):
                put("v", ("wv", n, s), [("ws", n, s)], widen, n, True, s)

        def wid(n, s):
            if n >= LAST:
                return [("ws", n, s)] + ([("wv", n, s)] if on_v(n, s) else [])
            return [("ws", n)] + ([("wv", n)] if on_v(n) else [])

        def I(n, s, eng="v"):
            put(eng, ("gr", n, s), wid(n, s), interleave, n, s, eng)

        def PI(n):
            put("t", ("il", n), wid(n, NOPE), pe_interleave, n)

        def E(n, eng="s"):
            put(eng, ("gr", n, NOPE), [("il", n)], pe_evacuate, n, eng)

        def Q(n, s):
            put("v", ("q", n, s), [("gr", n, ROPE if s == ROPE else NOPE)], quantize, n, s)

        def MR(n):
            put("t", ("mr", n), [("q", n, ROPE), ("xq",)], multiply, n, ROPE)

        def MN(n, ms=range(MT), s=NOPE):
            put("t", ("mn", n, s), [("q", n, s), ("xq",)], multiply, n, s, ms)

        def NP(q, m):
            put("t", ("np", q, m), [("q", G * q + g, NOPE) for g in range(G)] + [("xq",)], nope_passes, q, m)

        def NC(q, m, eng="s", s=NOPE):
            if q == QUADS - 1:
                needs = [("mn", LAST_NOPE[-1], s)]
            elif m < 2:
                needs = [("mn", G * q + G - 1, NOPE)]
            else:
                needs = [("np", q, m)]
            put(eng, ("nc", q, m, s), needs, nope_copy, q, m, eng, s)

        def XT(mp):
            put("t", ("xt", mp), [], x_turn, mp)

        def XO(mp, gs=range(G)):
            for g in gs:
                put("v", ("xo", mp, g), [("xt", mp)], x_out, mp, g)

        def XQ():
            put("v", ("xq",), [("xo", mp, g) for mp in range(2) for g in range(G)], x_quantize)

        def RM(q, m):
            put("v", ("rm", q, m), [("mr", G * q + G - 1), ("tab",)], rope_mul, q, m)

        def RA(q, m, eng="g"):
            put(eng, ("ra", q, m), [("rm", q, m)], rope_add, q, m, eng)

        def ST(q, m, lo, hi, s=NOPE):
            put("d", ("st", q, m, lo, s), ([("nc", q, m, s)] if lo == 0 else []) + ([("ra", q, m)] if hi == HD else []), store, q, m, lo, hi, s)

        for n in range(LAST):
            W(n)
            q, g = divmod(n, G)
            if n - ELAG in PE_BLOCKS:
                E(n - ELAG)
            if q >= 1 and g >= 2:
                NC(q - 1, 2 * g - 4)
                NC(q - 1, 2 * g - 3)
        for n in range(LAST - ELAG, LAST - 1):
            E(n)
        WH(12, ROPE)
        WH(13, ROPE)
        E(11)
        WH(14, ROPE)
        WH(15, ROPE)
        NC(2, 0)
        NC(2, 1)
        WH(12, NOPE)
        NC(2, 2)
        NC(2, 3)
        WH(13, NOPE)
        WH(14, NOPE)
        E(12)
        WH(15, NOPE)
        E(13)
        I(15, NOPE, "s")
        E(14)
        WV(0)
        WV(1)
        I(0, ROPE)
        I(0, NOPE)
        Q(0, ROPE)
        Q(0, NOPE)
        I(1, ROPE)
        WV(2)
        XO(0)
        Q(1, ROPE)
        I(2, ROPE)
        WV(3)
        XO(1)
        XQ()
        Q(1, NOPE)
        Q(2, ROPE)
        I(3, ROPE)
        WV(4)
        Q(2, NOPE)
        Q(3, ROPE)
        for q in range(1, QUADS - 1):
            u = G * q
            I(u, ROPE)
            WV(u + 1)
            Q(u - 1, NOPE)
            for m in range(MT):
                RM(q - 1, m)
            WV(u + 2)
            I(u, NOPE)
            Q(u, ROPE)
            I(u + 1, ROPE)
            Q(u, NOPE)
            Q(u + 1, ROPE)
            I(u + 2, ROPE)
            WV(u + 3)
            Q(u + 1, NOPE)
            Q(u + 2, ROPE)
            I(u + 3, ROPE)
            WV(u + 4)
            Q(u + 2, NOPE)
            Q(u + 3, ROPE)
        WVH(12, ROPE)
        WVH(13, ROPE)
        I(12, ROPE)
        Q(11, NOPE)
        WVH(14, ROPE)
        Q(12, ROPE)
        for m in range(MT):
            RM(2, m)
        I(13, ROPE)
        WVH(15, ROPE)
        I(14, ROPE)
        Q(13, ROPE)
        I(15, ROPE)
        Q(14, ROPE)
        Q(15, ROPE)
        WVH(14, NOPE)
        RM(3, 0)
        Q(12, "a")
        Q(12, "b")
        RM(3, 1)
        RM(3, 2)
        Q(13, "a")
        Q(13, "b")
        RM(3, 3)
        Q(15, "a")
        RA(3, 3, "v")
        Q(14, "a")
        Q(15, "b")
        Q(14, "b")
        NC(3, 1, "v", "a")
        NC(3, 3, "v", "a")
        NC(3, 0, "s", "a")
        NC(3, 2, "s", "a")
        for m in range(MT):
            NC(3, m, "v" if m % 2 else "s", "b")
        PI(1)
        XT(0)
        XT(1)
        PI(2)
        MR(0)
        MN(0, (0, 1))
        PI(3)
        MR(1)
        MN(1, (0, 1))
        MR(2)
        MR(3)
        for q in range(1, QUADS):
            u = G * q
            last = q == QUADS - 1
            MN(u - 2, (0, 1))
            MN(u - 1, (0, 1))
            if not last:
                PI(u + 1)
            NP(q - 1, 2)
            NP(q - 1, 3)
            if not last:
                PI(u + 2)
            MR(u)
            if not last:
                MN(u, (0, 1))
                PI(u + 3)
            else:
                PI(12)
            MR(u + 1)
            if not last:
                MN(u + 1, (0, 1))
            MR(u + 2)
            MR(u + 3)
        PI(13)
        MN(12, range(MT), "a")
        PI(14)
        MN(13, range(MT), "a")
        MN(15, range(MT), "a")
        MN(14, range(MT), "a")
        for n in LAST_NOPE:
            MN(n, range(MT), "b")
        put("g", ("tab",), [], tables)
        for q in range(QUADS):
            for m in range(MT):
                if (q, m) != (3, 3):
                    RA(q, m)
        for q in range(QUADS - 1):
            for m in range(MT):
                ST(q, m, 0, HD)
        for m in range(MT):
            ST(3, m, P, HD)
        for s in ("a", "b"):
            for m in range(MT):
                ST(3, m, 0, P, s)

        done = set()
        at = {e: 0 for e in progs}
        moved = True
        while moved:
            moved = False
            for e in ("s", "v", "t", "g", "d"):
                while at[e] < len(progs[e]):
                    gives, needs, fn, args = progs[e][at[e]]
                    if not all(k in done for k in needs):
                        break
                    fn(*args)
                    done.add(gives)
                    at[e] += 1
                    moved = True
        assert all(at[e] == len(progs[e]) for e in progs)
